import numpy as np
import ml_dtypes


def mxq(x, axis, fmt="e4m3"):
    dtype, down = {"e4m3": (ml_dtypes.float8_e4m3fn, 7), "e5m2": (ml_dtypes.float8_e5m2, 14)}[fmt]
    v = np.moveaxis(np.asarray(x, np.float32).astype(ml_dtypes.bfloat16).astype(np.float64), axis, -1)
    blocks = v.reshape(v.shape[:-1] + (-1, 32))
    amax = np.abs(blocks).max(-1, keepdims=True)
    byte = np.maximum(np.where(amax > 0, np.frexp(amax)[1] - 1 + 127, 0) - down, 1)
    scale = np.exp2(byte - 127.0)
    codes = (blocks / scale).astype(np.float32).astype(dtype).astype(np.float64)
    return np.moveaxis((codes * scale).reshape(v.shape), -1, axis)


WIDE = False


def mx_kscale(k):
    if not WIDE:
        return np.ones(k)
    levels = np.array([10, -10, 5, -5, 0])
    a = np.random.permutation(np.resize(levels, k // 512 * 4)).reshape(k // 512, 4)
    idx = np.arange(k)
    return np.exp2(a[idx // 512, idx % 128 // 32])


BF16 = ml_dtypes.bfloat16


def bf(x):
    return np.asarray(x, np.float32).astype(BF16)


def f64(x):
    return np.asarray(x).astype(np.float64)


B, T, D, H = 2, 512, 1024, 8
DH = D // H
NEG_BIG = -2.0**32 + 1.0
PAD = 0.125


def heads(t):
    return t.reshape(B, T, H, DH).transpose(2, 0, 1, 3)


def setup_inputs():
    s = mx_kscale(D)
    keep_q = np.random.random((B, T, H, 1)) >= PAD
    keep_k = np.random.random((B, T, H, 1)) >= PAD
    q = (np.random.standard_normal((B, T, H, DH)) * 1.25 * keep_q).reshape(B, T, D)
    k = (np.random.standard_normal((B, T, H, DH)) * 1.25 * keep_k).reshape(B, T, D)
    return {"Q": bf(q), "K": bf(k),
            "x": bf(np.random.standard_normal((B, T, D)) * s),
            "Wv": bf(np.random.standard_normal((D, D)) / np.sqrt(D) / s[None, :]),
            "mask": bf(np.random.random((B, T)) >= 0.2)}


def reference(Q, K, x, Wv, mask):
    Qh, Kh = heads(f64(Q)), heads(f64(K))
    V = mxq(f64(x), 2, "e4m3") @ mxq(f64(Wv), 1, "e4m3").T
    Vh = heads(V)
    scores = Qh @ Kh.transpose(0, 1, 3, 2) / np.sqrt(DH)
    key_masks = np.sign(np.abs(Kh).sum(-1))
    scores = np.where(key_masks[:, :, None, :] == 0, NEG_BIG, scores)
    dir_mask = np.triu(np.ones((T, T)), 1)
    scores = scores + (1.0 - dir_mask) * -10000.0
    e = np.exp(scores - scores.max(-1, keepdims=True))
    query_masks = np.sign(np.abs(Qh).sum(-1))
    out = (mxq(e, 3, "e4m3") @ mxq(Vh, 2, "e4m3")) / e.sum(-1, keepdims=True) * query_masks[..., None]
    out = out.transpose(1, 2, 0, 3).reshape(B, T, D)
    return out * f64(mask)[:, :, None]

@@ -1,0 +1,252 @@
+import math
+from contextlib import ExitStack
+
+import concourse.mybir as mybir
+from concourse.masks import make_identity
+
+F32 = mybir.dt.float32
+BF16 = mybir.dt.bfloat16
+U8 = mybir.dt.uint8
+U32 = mybir.dt.uint32
+I32 = mybir.dt.int32
+FP8X4 = mybir.dt.float8_e4m3fn_x4
+ALU = mybir.AluOpType
+ACT = mybir.ActivationFunctionType
+AX = mybir.AxisListType
+
+P = 128
+B, T, D, H = 2, 512, 1024, 8
+DH = D // H
+NB = T // P
+PACK = 4
+K_PASS = P * PACK
+G = D // K_PASS
+
+SCALE = 1.0 / math.sqrt(DH)
+ABSENT_KEY = (-(2.0**32) + 1.0) * math.sqrt(DH)
+EARLIER_KEY = -round(10000.0 * math.sqrt(DH) * 128.0) / 128.0
+
+NO_SIGN_BITS = 0x7FFF7FFF
+
+FLOPS = 2 * B * T * D * D + 2 * (2 * B * H * T * T * DH)
+
+
+def tile_multiheadattention_pa_kernel(tc, Q, K, x, Wv, mask, out):
+    nc = tc.nc
+    with ExitStack() as ctx:
+        keep = ctx.enter_context(tc.tile_pool(name="keep", bufs=1))
+        stage = ctx.enter_context(tc.tile_pool(name="stage", bufs=3))
+        soft = ctx.enter_context(tc.tile_pool(name="soft", bufs=2))
+        psum = ctx.enter_context(tc.psum_pool(name="psum", bufs=2))
+
+        ident_bf = keep.tile([P, P], BF16)
+        make_identity(nc, ident_bf[:])
+        ident_f32 = keep.tile([P, P], F32)
+        make_identity(nc, ident_f32[:])
+        tri = keep.tile([P, P], F32)
+        nc.gpsimd.memset(tri[:], EARLIER_KEY)
+        nc.gpsimd.affine_select(
+            out=tri[:], in_=tri[:], pattern=[[1, P]], compare_op=ALU.is_ge,
+            fill=0.0, base=0, channel_multiplier=-1,
+        )
+
+        k_nat = [keep.tile([P, NB, D], BF16, name="k_nat%d" % b) for b in range(B)]
+        q_nat = [keep.tile([P, NB, D], BF16, name="q_nat%d" % b) for b in range(B)]
+        x_nat = [keep.tile([P, 2, 2 * D], BF16, name="x_nat%d" % b) for b in range(B)]
+        w_nat = keep.tile([P, H, D], BF16)
+        w_rows = Wv.rearrange("(r p) k -> p r k", p=P)
+        for b in range(B):
+            nc.sync.dma_start(out=k_nat[b][:], in_=K[b].rearrange("(c p) d -> p c d", p=P))
+            nc.sync.dma_start(out=q_nat[b][:], in_=Q[b].rearrange("(c p) d -> p c d", p=P))
+            nc.sync.dma_start(
+                out=x_nat[b][:], in_=x[b].rearrange("(u p e) d -> p u (e d)", u=2, e=2)
+            )
+            half = slice(b * H // 2, (b + 1) * H // 2)
+            nc.sync.dma_start(out=w_nat[:, half, :], in_=w_rows[:, half, :])
+        mask_sb = keep.tile([P, B, NB], BF16)
+        with nc.allow_non_contiguous_dma(reason="1024 mask values, one to a partition and block"):
+            nc.sync.dma_start(out=mask_sb[:], in_=mask.rearrange("b (c p) -> p b c", p=P))
+
+        bits_k = keep.tile([P, B, NB * H], F32)
+        bits_q = keep.tile([P, B, NB * H], F32)
+        for b in range(B):
+            for nat, bits in ((k_nat[b], bits_k), (q_nat[b], bits_q)):
+                unsigned = stage.tile([P, NB * H, DH // 2], I32, bufs=2)
+                nc.vector.tensor_single_scalar(
+                    out=unsigned[:],
+                    in_=nat[:].bitcast(I32).rearrange("p c (h w) -> p (c h) w", h=H),
+                    scalar=NO_SIGN_BITS, op=ALU.bitwise_and,
+                )
+                nc.vector.tensor_reduce(out=bits[:, b, :], in_=unsigned[:], axis=AX.X, op=ALU.max)
+        later = keep.tile([P, B, NB, H], F32)
+        earlier = keep.tile([P, B, NB, H], F32)
+        nc.vector.tensor_scalar(
+            out=later[:].rearrange("p b c h -> p b (c h)"), in0=bits_k[:],
+            scalar1=0.0, scalar2=ABSENT_KEY,
+            op0=ALU.is_equal, op1=ALU.mult,
+        )
+        nc.vector.tensor_scalar_add(out=earlier[:], in0=later[:], scalar1=EARLIER_KEY)
+        row_on = keep.tile([P, B, NB, H], F32)
+        nc.vector.tensor_single_scalar(
+            out=row_on[:].rearrange("p b c h -> p b (c h)"), in_=bits_q[:], scalar=0.0, op=ALU.is_gt
+        )
+        nc.vector.tensor_tensor(
+            out=row_on[:], in0=row_on[:],
+            in1=mask_sb[:].unsqueeze(3).to_broadcast([P, B, NB, H]), op=ALU.mult,
+        )
+
+        kT = keep.tile([P, B, H, T], BF16)
+        qT = keep.tile([P, B, H, T], BF16)
+        for b in range(B):
+            for nat, turned_sb in ((k_nat[b], kT), (q_nat[b], qT)):
+                for h0 in range(0, H, 2):
+                    turned = psum.tile([P, 2, T], BF16, tag="scores", bufs=4)
+                    for hh in range(2):
+                        for c in range(NB):
+                            nc.tensor.transpose(
+                                out=turned[:, hh, c * P:(c + 1) * P],
+                                in_=nat[:, c, (h0 + hh) * DH:(h0 + hh + 1) * DH],
+                                identity=ident_bf[:],
+                            )
+                    nc.scalar.copy(out=turned_sb[:, b, h0:h0 + 2, :], in_=turned[:])
+
+        def pack_rows(words, codes, scales):
+            turned = psum.tile([P, G * 2, P], F32, tag="scores", bufs=4)
+            for q in range(G * 2):
+                nc.tensor.transpose(
+                    out=turned[:, q, :], in_=words[:, q * P:(q + 1) * P], identity=ident_f32[:]
+                )
+            grouped = stage.tile([P, G, P, PACK], BF16, align_bytes=64)
+            nc.scalar.copy(
+                out=grouped[:].bitcast(F32),
+                in_=turned[:].rearrange("p (g u) r -> p g r u", g=G),
+            )
+            nc.vector.quantize_mx(
+                out=codes.bitcast(FP8X4), scales=scales,
+                in_=grouped[:].rearrange("p g r t -> p (g r t)"),
+            )
+
+        x_codes = keep.tile([P, B * PACK, G * P], U32, align_bytes=64)
+        x_scales = keep.tile([P, B * PACK, G * P], U8, align_bytes=64)
+        w_codes = keep.tile([P, H, G * P], U32, align_bytes=64)
+        w_scales = keep.tile([P, H, G * P], U8, align_bytes=64)
+        v_codes = keep.tile([P, B * H, DH], U32, align_bytes=64)
+        v_scales = keep.tile([P, B * H, DH], U8, align_bytes=64)
+        for b in range(B):
+            x_words = x_nat[b][:].bitcast(F32)
+            for t in range(PACK):
+                u, e = divmod(t, 2)
+                pack_rows(
+                    x_words[:, u, e * (D // 2):(e + 1) * (D // 2)],
+                    x_codes[:, b * PACK + t, :], x_scales[:, b * PACK + t, :],
+                )
+            w_words = w_nat[:].bitcast(F32)
+            for r in range(b * H // 2, (b + 1) * H // 2):
+                pack_rows(w_words[:, r, :], w_codes[:, r, :], w_scales[:, r, :])
+
+        HEADS_AT_ONCE = 4
+        for b in range(B):
+            for h0 in range(0, H, HEADS_AT_ONCE):
+                v_grouped = stage.tile([P, HEADS_AT_ONCE, DH, PACK], BF16, align_bytes=64)
+                for hh in range(HEADS_AT_ONCE):
+                    h = h0 + hh
+                    v_acc = psum.tile([P, PACK, DH], F32, tag="turned", bufs=2)
+                    for t in range(PACK):
+                        for g in range(G):
+                            cols = slice(g * P, (g + 1) * P)
+                            nc.tensor.matmul_mx(
+                                out=v_acc[:, t, :],
+                                lhsT=x_codes[:, b * PACK + t, cols].bitcast(FP8X4),
+                                lhsT_scale=x_scales[:, b * PACK + t, cols],
+                                rhs=w_codes[:, h, cols].bitcast(FP8X4),
+                                rhs_scale=w_scales[:, h, cols],
+                                start=(g == 0), stop=(g == G - 1),
+                            )
+                    copy_out = nc.scalar.copy if hh % 2 == 0 else nc.vector.tensor_copy
+                    copy_out(out=v_grouped[:, hh, :, :], in_=v_acc[:].rearrange("p t d -> p d t"))
+                heads = slice(b * H + h0, b * H + h0 + HEADS_AT_ONCE)
+                nc.vector.quantize_mx(
+                    out=v_codes[:, heads, :].rearrange("p h d -> p (h d)").bitcast(FP8X4),
+                    scales=v_scales[:, heads, :].rearrange("p h d -> p (h d)"),
+                    in_=v_grouped[:].rearrange("p h d t -> p (h d t)"),
+                )
+
+        for b in range(B):
+            out_rows = out[b].rearrange("(i p) (h d) -> p i h d", p=P, h=H)
+            for h in range(H):
+                diag = soft.tile([P, NB, P], F32)
+                nc.gpsimd.tensor_tensor(
+                    out=diag[:], in0=tri[:].unsqueeze(1).to_broadcast([P, NB, P]),
+                    in1=later[:, b, :, h:h + 1].to_broadcast([P, NB, P]), op=ALU.add,
+                )
+                e_sb = soft.tile([P, NB, T], BF16)
+                shift = soft.tile([P, NB], F32)
+                rowsum = soft.tile([P, NB], F32)
+                for i in range(NB):
+                    scores = psum.tile([P, T], F32, tag="scores", bufs=4)
+                    nc.tensor.matmul(
+                        out=scores[:], lhsT=qT[:, b, h, i * P:(i + 1) * P], rhs=kT[:, b, h, :],
+                        start=True, stop=False,
+                    )
+                    for j in range(NB):
+                        if j == i:
+                            addend = diag[:, j, :]
+                        elif j < i:
+                            addend = earlier[:, b, j, h:h + 1].to_broadcast([P, P])
+                        else:
+                            addend = later[:, b, j, h:h + 1].to_broadcast([P, P])
+                        nc.tensor.matmul(
+                            out=scores[:, j * P:(j + 1) * P], lhsT=addend, rhs=ident_f32[:],
+                            is_transpose=True, start=False, stop=(j == NB - 1),
+                        )
+                    negated = soft.tile([P, T], F32, bufs=4)
+                    nc.vector.tensor_scalar(
+                        out=negated[:], in0=scores[:], scalar1=-SCALE, scalar2=None,
+                        op0=ALU.mult, op1=ALU.min, accum_out=shift[:, i:i + 1],
+                    )
+                    nc.scalar.activation(
+                        out=e_sb[:, i, :], in_=negated[:], func=ACT.Exp,
+                        bias=shift[:, i:i + 1], scale=-1.0, accum_out=rowsum[:, i:i + 1],
+                    )
+                e_words = e_sb[:].bitcast(F32)
+                e_grouped = soft.tile([P, NB * P, PACK], BF16, align_bytes=64)
+                for i0 in range(0, NB, 2):
+                    e_turned = psum.tile([P, 2, 2 * P], F32, tag="turned", bufs=2)
+                    for u in range(2):
+                        for ii in range(2):
+                            nc.tensor.transpose(
+                                out=e_turned[:, u, ii * P:(ii + 1) * P],
+                                in_=e_words[:, i0 + ii, u * P:(u + 1) * P],
+                                identity=ident_f32[:],
+                            )
+                    nc.scalar.copy(
+                        out=e_grouped[:, i0 * P:(i0 + 2) * P, :].bitcast(F32),
+                        in_=e_turned[:].rearrange("p u i -> p i u"),
+                    )
+                e_codes = soft.tile([P, NB * P], U32, align_bytes=64)
+                e_scales = soft.tile([P, NB * P], U8, align_bytes=64)
+                nc.vector.quantize_mx(
+                    out=e_codes[:].bitcast(FP8X4), scales=e_scales[:],
+                    in_=e_grouped[:].rearrange("p i t -> p (i t)"),
+                )
+                o_acc = psum.tile([P, NB, DH], F32, tag="o_acc", bufs=2)
+                for i in range(NB):
+                    nc.tensor.matmul_mx(
+                        out=o_acc[:, i, :],
+                        lhsT=e_codes[:, i * P:(i + 1) * P].bitcast(FP8X4),
+                        lhsT_scale=e_scales[:, i * P:(i + 1) * P],
+                        rhs=v_codes[:, b * H + h, :].bitcast(FP8X4),
+                        rhs_scale=v_scales[:, b * H + h, :],
+                        start=True, stop=True,
+                    )
+                factor = soft.tile([P, NB], F32)
+                nc.vector.reciprocal(out=factor[:], in_=rowsum[:])
+                nc.vector.tensor_tensor(
+                    out=factor[:], in0=factor[:], in1=row_on[:, b, :, h], op=ALU.mult
+                )
+                o_sb = soft.tile([P, NB, DH], F32, bufs=3)
+                nc.vector.tensor_tensor(
+                    out=o_sb[:], in0=o_acc[:],
+                    in1=factor[:].unsqueeze(2).to_broadcast([P, NB, DH]), op=ALU.mult,
+                )
+                nc.sync.dma_start(out=out_rows[:, :, h, :], in_=o_sb[:])

@@ -43,10 +43,11 @@ def tile_multiheadattention_pa_kernel(tc, Q, K, x, Wv, mask, out):
         make_identity(nc, ident_bf[:])
         ident_f32 = keep.tile([P, P], F32)
         make_identity(nc, ident_f32[:])
-        tri = keep.tile([P, P], F32)
-        nc.gpsimd.memset(tri[:], EARLIER_KEY)
+        causal = keep.tile([P, 3, P], F32)
+        nc.gpsimd.memset(causal[:, 0:2, :], EARLIER_KEY)
+        nc.gpsimd.memset(causal[:, 2, :], 0.0)
         nc.gpsimd.affine_select(
-            out=tri[:], in_=tri[:], pattern=[[1, P]], compare_op=ALU.is_ge,
+            out=causal[:, 1, :], in_=causal[:, 1, :], pattern=[[1, P]], compare_op=ALU.is_ge,
             fill=0.0, base=0, channel_multiplier=-1,
         )
 
@@ -79,13 +80,11 @@ def tile_multiheadattention_pa_kernel(tc, Q, K, x, Wv, mask, out):
                 )
                 nc.vector.tensor_reduce(out=bits[:, b, :], in_=unsigned[:], axis=AX.X, op=ALU.max)
         later = keep.tile([P, B, NB, H], F32)
-        earlier = keep.tile([P, B, NB, H], F32)
         nc.vector.tensor_scalar(
             out=later[:].rearrange("p b c h -> p b (c h)"), in0=bits_k[:],
             scalar1=0.0, scalar2=ABSENT_KEY,
             op0=ALU.is_equal, op1=ALU.mult,
         )
-        nc.vector.tensor_scalar_add(out=earlier[:], in0=later[:], scalar1=EARLIER_KEY)
         row_on = keep.tile([P, B, NB, H], F32)
         nc.vector.tensor_single_scalar(
             out=row_on[:].rearrange("p b c h -> p b (c h)"), in_=bits_q[:], scalar=0.0, op=ALU.is_gt
@@ -174,11 +173,14 @@ def tile_multiheadattention_pa_kernel(tc, Q, K, x, Wv, mask, out):
         for b in range(B):
             out_rows = out[b].rearrange("(i p) (h d) -> p i h d", p=P, h=H)
             for h in range(H):
-                diag = soft.tile([P, NB, P], F32)
-                nc.gpsimd.tensor_tensor(
-                    out=diag[:], in0=tri[:].unsqueeze(1).to_broadcast([P, NB, P]),
-                    in1=later[:, b, :, h:h + 1].to_broadcast([P, NB, P]), op=ALU.add,
-                )
+                addends = soft.tile([P, NB, 3, P], F32, bufs=3)
+                for j in range(NB):
+                    kinds = slice(1 if j == NB - 1 else 0, 2 if j == 0 else 3)
+                    nc.gpsimd.tensor_scalar(
+                        out=addends[:, j, kinds, :], in0=causal[:, kinds, :],
+                        scalar1=1.0, scalar2=later[:, b, j, h:h + 1],
+                        op0=ALU.mult, op1=ALU.add,
+                    )
                 e_sb = soft.tile([P, NB, T], BF16)
                 shift = soft.tile([P, NB], F32)
                 rowsum = soft.tile([P, NB], F32)
@@ -189,14 +191,10 @@ def tile_multiheadattention_pa_kernel(tc, Q, K, x, Wv, mask, out):
                         start=True, stop=False,
                     )
                     for j in range(NB):
-                        if j == i:
-                            addend = diag[:, j, :]
-                        elif j < i:
-                            addend = earlier[:, b, j, h:h + 1].to_broadcast([P, P])
-                        else:
-                            addend = later[:, b, j, h:h + 1].to_broadcast([P, P])
+                        kind = 0 if j < i else 1 if j == i else 2
                         nc.tensor.matmul(
-                            out=scores[:, j * P:(j + 1) * P], lhsT=addend, rhs=ident_f32[:],
+                            out=scores[:, j * P:(j + 1) * P], lhsT=addends[:, j, kind, :],
+                            rhs=ident_f32[:],
                             is_transpose=True, start=False, stop=(j == NB - 1),
                         )
                     negated = soft.tile([P, T], F32, bufs=4)

@@ -21,6 +21,8 @@ NB = T // P
 PACK = 4
 K_PASS = P * PACK
 G = D // K_PASS
+HALF = H // 2
+PAIRS = H // 2
 
 SCALE = 1.0 / math.sqrt(DH)
 ABSENT_KEY = (-(2.0**32) + 1.0) * math.sqrt(DH)
@@ -51,200 +53,382 @@ def tile_multiheadattention_pa_kernel(tc, Q, K, x, Wv, mask, out):
             fill=0.0, base=0, channel_multiplier=-1,
         )
 
-        k_nat = [keep.tile([P, NB, D], BF16, name="k_nat%d" % b) for b in range(B)]
-        q_nat = [keep.tile([P, NB, D], BF16, name="q_nat%d" % b) for b in range(B)]
-        x_nat = [keep.tile([P, 2, 2 * D], BF16, name="x_nat%d" % b) for b in range(B)]
-        w_nat = keep.tile([P, H, D], BF16)
-        w_rows = Wv.rearrange("(r p) k -> p r k", p=P)
+        ctx.enter_context(tc.manual_schedule())
+
+        k_nat = {}
+        q_nat = {}
+        x_nat = {}
+        w_nat = {}
         for b in range(B):
-            nc.sync.dma_start(out=k_nat[b][:], in_=K[b].rearrange("(c p) d -> p c d", p=P))
-            nc.sync.dma_start(out=q_nat[b][:], in_=Q[b].rearrange("(c p) d -> p c d", p=P))
+            x_nat[b] = keep.tile([P, 2, 2 * D], BF16, name="x_nat%d" % b)
+            for f in range(2):
+                k_nat[b, f] = keep.tile([P, NB, D // 2], BF16, name="k_nat%d%d" % (b, f))
+                q_nat[b, f] = keep.tile([P, NB, D // 2], BF16, name="q_nat%d%d" % (b, f))
+        for f in range(2):
+            w_nat[f] = keep.tile([P, HALF, D], BF16, name="w_nat%d" % f)
+        mask_sb = keep.tile([P, B, NB], BF16)
+
+        def load_heads(b, f):
+            cols = slice(f * D // 2, (f + 1) * D // 2)
+            for nat, src in ((k_nat, K), (q_nat, Q)):
+                nc.sync.dma_start(
+                    out=nat[b, f][:], in_=src[b].rearrange("(c p) d -> p c d", p=P)[:, :, cols]
+                )
+
+        def load_x(b):
             nc.sync.dma_start(
                 out=x_nat[b][:], in_=x[b].rearrange("(u p e) d -> p u (e d)", u=2, e=2)
             )
-            half = slice(b * H // 2, (b + 1) * H // 2)
-            nc.sync.dma_start(out=w_nat[:, half, :], in_=w_rows[:, half, :])
-        mask_sb = keep.tile([P, B, NB], BF16)
+
+        def load_w(f):
+            nc.sync.dma_start(
+                out=w_nat[f][:],
+                in_=Wv.rearrange("(r p) k -> p r k", p=P)[:, f * HALF:(f + 1) * HALF, :],
+            )
+
+        load_heads(0, 0)
+        load_x(0)
+        load_w(0)
+        load_heads(0, 1)
         with nc.allow_non_contiguous_dma(reason="1024 mask values, one to a partition and block"):
             nc.sync.dma_start(out=mask_sb[:], in_=mask.rearrange("b (c p) -> p b c", p=P))
+        load_w(1)
+        load_heads(1, 0)
+        load_x(1)
+        load_heads(1, 1)
 
-        bits_k = keep.tile([P, B, NB * H], F32)
-        bits_q = keep.tile([P, B, NB * H], F32)
-        for b in range(B):
-            for nat, bits in ((k_nat[b], bits_k), (q_nat[b], bits_q)):
-                unsigned = stage.tile([P, NB * H, DH // 2], I32, bufs=2)
-                nc.vector.tensor_single_scalar(
-                    out=unsigned[:],
-                    in_=nat[:].bitcast(I32).rearrange("p c (h w) -> p (c h) w", h=H),
-                    scalar=NO_SIGN_BITS, op=ALU.bitwise_and,
-                )
-                nc.vector.tensor_reduce(out=bits[:, b, :], in_=unsigned[:], axis=AX.X, op=ALU.max)
-        later = keep.tile([P, B, NB, H], F32)
-        nc.vector.tensor_scalar(
-            out=later[:].rearrange("p b c h -> p b (c h)"), in0=bits_k[:],
-            scalar1=0.0, scalar2=ABSENT_KEY,
-            op0=ALU.is_equal, op1=ALU.mult,
-        )
-        row_on = keep.tile([P, B, NB, H], F32)
-        nc.vector.tensor_single_scalar(
-            out=row_on[:].rearrange("p b c h -> p b (c h)"), in_=bits_q[:], scalar=0.0, op=ALU.is_gt
-        )
-        nc.vector.tensor_tensor(
-            out=row_on[:], in0=row_on[:],
-            in1=mask_sb[:].unsqueeze(3).to_broadcast([P, B, NB, H]), op=ALU.mult,
-        )
+        later = {}
+        row_on = {}
+        unsigned = {}
 
-        kT = keep.tile([P, B, H, T], BF16)
-        qT = keep.tile([P, B, H, T], BF16)
-        for b in range(B):
-            for nat, turned_sb in ((k_nat[b], kT), (q_nat[b], qT)):
-                for h0 in range(0, H, 2):
-                    turned = psum.tile([P, 2, T], BF16, tag="scores", bufs=4)
-                    for hh in range(2):
-                        for c in range(NB):
-                            nc.tensor.transpose(
-                                out=turned[:, hh, c * P:(c + 1) * P],
-                                in_=nat[:, c, (h0 + hh) * DH:(h0 + hh + 1) * DH],
-                                identity=ident_bf[:],
-                            )
-                    nc.scalar.copy(out=turned_sb[:, b, h0:h0 + 2, :], in_=turned[:])
-
-        def pack_rows(words, codes, scales):
-            turned = psum.tile([P, G * 2, P], F32, tag="scores", bufs=4)
-            for q in range(G * 2):
-                nc.tensor.transpose(
-                    out=turned[:, q, :], in_=words[:, q * P:(q + 1) * P], identity=ident_f32[:]
-                )
-            grouped = stage.tile([P, G, P, PACK], BF16, align_bytes=64)
-            nc.scalar.copy(
-                out=grouped[:].bitcast(F32),
-                in_=turned[:].rearrange("p (g u) r -> p g r u", g=G),
-            )
-            nc.vector.quantize_mx(
-                out=codes.bitcast(FP8X4), scales=scales,
-                in_=grouped[:].rearrange("p g r t -> p (g r t)"),
+        def clear_signs(nat, b, f):
+            unsigned[b, f] = stage.tile([P, NB * HALF, DH // 2], I32, bufs=2, name="unsigned")
+            nc.vector.tensor_single_scalar(
+                out=unsigned[b, f][:],
+                in_=nat[b, f][:].bitcast(I32).rearrange("p c (h w) -> p (c h) w", h=HALF),
+                scalar=NO_SIGN_BITS, op=ALU.bitwise_and,
             )
 
-        x_codes = keep.tile([P, B * PACK, G * P], U32, align_bytes=64)
-        x_scales = keep.tile([P, B * PACK, G * P], U8, align_bytes=64)
+        def find_keys(b, f):
+            bits = stage.tile([P, NB * HALF], F32, bufs=2)
+            nc.vector.tensor_reduce(out=bits[:], in_=unsigned[b, f][:], axis=AX.X, op=ALU.max)
+            later[b, f] = keep.tile([P, NB, HALF], F32, name="later%d%d" % (b, f))
+            nc.vector.tensor_scalar(
+                out=later[b, f][:].rearrange("p c h -> p (c h)"), in0=bits[:],
+                scalar1=0.0, scalar2=ABSENT_KEY, op0=ALU.is_equal, op1=ALU.mult,
+            )
+
+        def find_queries(b, f):
+            bits = stage.tile([P, NB * HALF], F32, bufs=2)
+            nc.vector.tensor_reduce(out=bits[:], in_=unsigned[b, f][:], axis=AX.X, op=ALU.max)
+            row_on[b, f] = keep.tile([P, NB, HALF], F32, name="row_on%d%d" % (b, f))
+            nc.vector.tensor_single_scalar(
+                out=row_on[b, f][:].rearrange("p c h -> p (c h)"), in_=bits[:],
+                scalar=0.0, op=ALU.is_gt,
+            )
+            nc.vector.tensor_tensor(
+                out=row_on[b, f][:], in0=row_on[b, f][:],
+                in1=mask_sb[:, b, :].unsqueeze(2).to_broadcast([P, NB, HALF]), op=ALU.mult,
+            )
+
+        kT = {}
+        qT = {}
+        x_codes = {}
+        x_scales = {}
+        for b in range(B):
+            x_codes[b] = keep.tile([P, PACK, G * P], U32, align_bytes=64, name="x_codes%d" % b)
+            x_scales[b] = keep.tile([P, PACK, G * P], U8, align_bytes=64, name="x_scales%d" % b)
         w_codes = keep.tile([P, H, G * P], U32, align_bytes=64)
         w_scales = keep.tile([P, H, G * P], U8, align_bytes=64)
         v_codes = keep.tile([P, B * H, DH], U32, align_bytes=64)
         v_scales = keep.tile([P, B * H, DH], U8, align_bytes=64)
-        for b in range(B):
-            x_words = x_nat[b][:].bitcast(F32)
-            for t in range(PACK):
-                u, e = divmod(t, 2)
-                pack_rows(
-                    x_words[:, u, e * (D // 2):(e + 1) * (D // 2)],
-                    x_codes[:, b * PACK + t, :], x_scales[:, b * PACK + t, :],
-                )
-            w_words = w_nat[:].bitcast(F32)
-            for r in range(b * H // 2, (b + 1) * H // 2):
-                pack_rows(w_words[:, r, :], w_codes[:, r, :], w_scales[:, r, :])
 
-        HEADS_AT_ONCE = 4
-        for b in range(B):
-            for h0 in range(0, H, HEADS_AT_ONCE):
-                v_grouped = stage.tile([P, HEADS_AT_ONCE, DH, PACK], BF16, align_bytes=64)
-                for hh in range(HEADS_AT_ONCE):
-                    h = h0 + hh
-                    v_acc = psum.tile([P, PACK, DH], F32, tag="turned", bufs=2)
-                    for t in range(PACK):
-                        for g in range(G):
-                            cols = slice(g * P, (g + 1) * P)
-                            nc.tensor.matmul_mx(
-                                out=v_acc[:, t, :],
-                                lhsT=x_codes[:, b * PACK + t, cols].bitcast(FP8X4),
-                                lhsT_scale=x_scales[:, b * PACK + t, cols],
-                                rhs=w_codes[:, h, cols].bitcast(FP8X4),
-                                rhs_scale=w_scales[:, h, cols],
-                                start=(g == 0), stop=(g == G - 1),
-                            )
-                    copy_out = nc.scalar.copy if hh % 2 == 0 else nc.vector.tensor_copy
-                    copy_out(out=v_grouped[:, hh, :, :], in_=v_acc[:].rearrange("p t d -> p d t"))
-                heads = slice(b * H + h0, b * H + h0 + HEADS_AT_ONCE)
-                nc.vector.quantize_mx(
-                    out=v_codes[:, heads, :].rearrange("p h d -> p (h d)").bitcast(FP8X4),
-                    scales=v_scales[:, heads, :].rearrange("p h d -> p (h d)"),
-                    in_=v_grouped[:].rearrange("p h d t -> p (h d t)"),
-                )
+        def turn_unit(nat, turned_sb, b, pair):
+            f, first = divmod(2 * pair, HALF)
+            held = {}
 
-        for b in range(B):
-            out_rows = out[b].rearrange("(i p) (h d) -> p i h d", p=P, h=H)
-            for h in range(H):
-                addends = soft.tile([P, NB, 3, P], F32, bufs=3)
-                for j in range(NB):
-                    kinds = slice(1 if j == NB - 1 else 0, 2 if j == 0 else 3)
-                    nc.gpsimd.tensor_scalar(
-                        out=addends[:, j, kinds, :], in0=causal[:, kinds, :],
-                        scalar1=1.0, scalar2=later[:, b, j, h:h + 1],
-                        op0=ALU.mult, op1=ALU.add,
-                    )
-                e_sb = soft.tile([P, NB, T], BF16)
-                shift = soft.tile([P, NB], F32)
-                rowsum = soft.tile([P, NB], F32)
-                for i in range(NB):
-                    scores = psum.tile([P, T], F32, tag="scores", bufs=4)
-                    nc.tensor.matmul(
-                        out=scores[:], lhsT=qT[:, b, h, i * P:(i + 1) * P], rhs=kT[:, b, h, :],
-                        start=True, stop=False,
-                    )
-                    for j in range(NB):
-                        kind = 0 if j < i else 1 if j == i else 2
-                        nc.tensor.matmul(
-                            out=scores[:, j * P:(j + 1) * P], lhsT=addends[:, j, kind, :],
-                            rhs=ident_f32[:],
-                            is_transpose=True, start=False, stop=(j == NB - 1),
+            def fill():
+                held["psum"] = psum.tile([P, 2, T], BF16, tag="turned", bufs=3, name="turned")
+                for hh in range(2):
+                    for c in range(NB):
+                        nc.tensor.transpose(
+                            out=held["psum"][:, hh, c * P:(c + 1) * P],
+                            in_=nat[b, f][:, c, (first + hh) * DH:(first + hh + 1) * DH],
+                            identity=ident_bf[:],
                         )
-                    negated = soft.tile([P, T], F32, bufs=4)
-                    nc.vector.tensor_scalar(
-                        out=negated[:], in0=scores[:], scalar1=-SCALE, scalar2=None,
-                        op0=ALU.mult, op1=ALU.min, accum_out=shift[:, i:i + 1],
+
+            def copy():
+                which = "kT" if nat is k_nat else "qT"
+                turned_sb[b, pair] = keep.tile([P, 2, T], BF16, name="%s%d%d" % (which, b, pair))
+                nc.scalar.copy(out=turned_sb[b, pair][:], in_=held["psum"][:])
+
+            return [fill, copy]
+
+        def pack_unit(words, codes, scales):
+            held = {}
+
+            def fill():
+                held["psum"] = psum.tile([P, G * 2, P], F32, tag="turned", bufs=3, name="turned")
+                for q in range(G * 2):
+                    nc.tensor.transpose(
+                        out=held["psum"][:, q, :], in_=words[:, q * P:(q + 1) * P],
+                        identity=ident_f32[:],
                     )
-                    nc.scalar.activation(
-                        out=e_sb[:, i, :], in_=negated[:], func=ACT.Exp,
-                        bias=shift[:, i:i + 1], scale=-1.0, accum_out=rowsum[:, i:i + 1],
-                    )
-                e_words = e_sb[:].bitcast(F32)
-                e_grouped = soft.tile([P, NB * P, PACK], BF16, align_bytes=64)
-                for i0 in range(0, NB, 2):
-                    e_turned = psum.tile([P, 2, 2 * P], F32, tag="turned", bufs=2)
-                    for u in range(2):
-                        for ii in range(2):
-                            nc.tensor.transpose(
-                                out=e_turned[:, u, ii * P:(ii + 1) * P],
-                                in_=e_words[:, i0 + ii, u * P:(u + 1) * P],
-                                identity=ident_f32[:],
-                            )
-                    nc.scalar.copy(
-                        out=e_grouped[:, i0 * P:(i0 + 2) * P, :].bitcast(F32),
-                        in_=e_turned[:].rearrange("p u i -> p i u"),
-                    )
-                e_codes = soft.tile([P, NB * P], U32, align_bytes=64)
-                e_scales = soft.tile([P, NB * P], U8, align_bytes=64)
+
+            def copy():
+                held["sb"] = stage.tile([P, G, P, PACK], BF16, align_bytes=64, name="grouped")
+                nc.scalar.copy(
+                    out=held["sb"][:].bitcast(F32),
+                    in_=held["psum"][:].rearrange("p (g u) r -> p g r u", g=G),
+                )
+
+            def quantise():
                 nc.vector.quantize_mx(
-                    out=e_codes[:].bitcast(FP8X4), scales=e_scales[:],
-                    in_=e_grouped[:].rearrange("p i t -> p (i t)"),
+                    out=codes.bitcast(FP8X4), scales=scales,
+                    in_=held["sb"][:].rearrange("p g r t -> p (g r t)"),
                 )
-                o_acc = psum.tile([P, NB, DH], F32, tag="o_acc", bufs=2)
-                for i in range(NB):
-                    nc.tensor.matmul_mx(
-                        out=o_acc[:, i, :],
-                        lhsT=e_codes[:, i * P:(i + 1) * P].bitcast(FP8X4),
-                        lhsT_scale=e_scales[:, i * P:(i + 1) * P],
-                        rhs=v_codes[:, b * H + h, :].bitcast(FP8X4),
-                        rhs_scale=v_scales[:, b * H + h, :],
-                        start=True, stop=True,
+
+            return [fill, copy, quantise]
+
+        def x_unit(b, t):
+            u, e = divmod(t, 2)
+            words = x_nat[b][:].bitcast(F32)[:, u, e * (D // 2):(e + 1) * (D // 2)]
+            return pack_unit(words, x_codes[b][:, t, :], x_scales[b][:, t, :])
+
+        def w_unit(r):
+            f, row = divmod(r, HALF)
+            return pack_unit(w_nat[f][:].bitcast(F32)[:, row, :], w_codes[:, r, :], w_scales[:, r, :])
+
+        v_ready = {}
+
+        def v_unit(b, h):
+            held = {}
+
+            def fill():
+                held["psum"] = psum.tile([P, PACK, DH], F32, tag="sums", bufs=2, name="v_acc")
+                for t in range(PACK):
+                    for g in range(G):
+                        cols = slice(g * P, (g + 1) * P)
+                        nc.tensor.matmul_mx(
+                            out=held["psum"][:, t, :],
+                            lhsT=x_codes[b][:, t, cols].bitcast(FP8X4),
+                            lhsT_scale=x_scales[b][:, t, cols],
+                            rhs=w_codes[:, h, cols].bitcast(FP8X4),
+                            rhs_scale=w_scales[:, h, cols],
+                            start=(g == 0), stop=(g == G - 1),
+                        )
+
+            def copy():
+                held["sb"] = stage.tile([P, DH, PACK], BF16, align_bytes=64, name="v_grouped")
+                nc.scalar.copy(
+                    out=held["sb"][:], in_=held["psum"][:].rearrange("p t d -> p d t")
+                )
+
+            def quantise():
+                nc.vector.quantize_mx(
+                    out=v_codes[:, b * H + h, :].bitcast(FP8X4), scales=v_scales[:, b * H + h, :],
+                    in_=held["sb"][:].rearrange("p d t -> p (d t)"),
+                )
+                v_ready[b, h] = True
+
+            return [fill, copy, quantise]
+
+        addends = {}
+        e_sb = {}
+        shift = {}
+        rowsum = {}
+        negated = {}
+        e_turned = {}
+        e_grouped = {}
+        e_codes = {}
+        e_scales = {}
+        factor = {}
+        scores = {}
+        o_acc = {}
+
+        def make_addends(n):
+            b, h = divmod(n, H)
+            f, hf = divmod(h, HALF)
+            addends[n] = soft.tile([P, NB, 3, P], F32, bufs=3, name="addends")
+            for j in range(NB):
+                kinds = slice(1 if j == NB - 1 else 0, 2 if j == 0 else 3)
+                nc.gpsimd.tensor_scalar(
+                    out=addends[n][:, j, kinds, :], in0=causal[:, kinds, :],
+                    scalar1=1.0, scalar2=later[b, f][:, j, hf:hf + 1],
+                    op0=ALU.mult, op1=ALU.add,
+                )
+
+        def score(n, i):
+            b, h = divmod(n, H)
+            pair, hh = divmod(h, 2)
+            scores[n, i] = psum.tile([P, T], F32, tag="scores", bufs=3, name="scores")
+            nc.tensor.matmul(
+                out=scores[n, i][:], lhsT=qT[b, pair][:, hh, i * P:(i + 1) * P],
+                rhs=kT[b, pair][:, hh, :], start=True, stop=False,
+            )
+            for j in range(NB):
+                kind = 0 if j < i else 1 if j == i else 2
+                nc.tensor.matmul(
+                    out=scores[n, i][:, j * P:(j + 1) * P], lhsT=addends[n][:, j, kind, :],
+                    rhs=ident_f32[:], is_transpose=True, start=False, stop=(j == NB - 1),
+                )
+
+        def negate(n, i):
+            if i == 0:
+                shift[n] = soft.tile([P, NB], F32, bufs=3, name="shift")
+            negated[n, i] = soft.tile([P, T], F32, bufs=4, name="negated")
+            nc.vector.tensor_scalar(
+                out=negated[n, i][:], in0=scores[n, i][:], scalar1=-SCALE, scalar2=None,
+                op0=ALU.mult, op1=ALU.min, accum_out=shift[n][:, i:i + 1],
+            )
+
+        def exponent(n, i):
+            if i == 0:
+                e_sb[n] = soft.tile([P, NB, T], BF16, bufs=3, name="e_sb")
+                rowsum[n] = soft.tile([P, NB], F32, bufs=4, name="rowsum")
+            nc.scalar.activation(
+                out=e_sb[n][:, i, :], in_=negated[n, i][:], func=ACT.Exp,
+                bias=shift[n][:, i:i + 1], scale=-1.0, accum_out=rowsum[n][:, i:i + 1],
+            )
+
+        def turn_e(n, half):
+            words = e_sb[n][:].bitcast(F32)
+            e_turned[n, half] = psum.tile([P, 2, 2 * P], F32, tag="turned", bufs=3, name="turned")
+            for u in range(2):
+                for ii in range(2):
+                    nc.tensor.transpose(
+                        out=e_turned[n, half][:, u, ii * P:(ii + 1) * P],
+                        in_=words[:, 2 * half + ii, u * P:(u + 1) * P],
+                        identity=ident_f32[:],
                     )
-                factor = soft.tile([P, NB], F32)
-                nc.vector.reciprocal(out=factor[:], in_=rowsum[:])
-                nc.vector.tensor_tensor(
-                    out=factor[:], in0=factor[:], in1=row_on[:, b, :, h], op=ALU.mult
+
+        def copy_e(n, half):
+            if half == 0:
+                e_grouped[n] = soft.tile([P, NB * P, PACK], BF16, align_bytes=64, bufs=3, name="e_grouped")
+            nc.scalar.copy(
+                out=e_grouped[n][:, half * 2 * P:(half + 1) * 2 * P, :].bitcast(F32),
+                in_=e_turned[n, half][:].rearrange("p u i -> p i u"),
+            )
+
+        def quantise_e(n):
+            e_codes[n] = soft.tile([P, NB * P], U32, align_bytes=64, bufs=4, name="e_codes")
+            e_scales[n] = soft.tile([P, NB * P], U8, align_bytes=64, bufs=4, name="e_scales")
+            nc.vector.quantize_mx(
+                out=e_codes[n][:].bitcast(FP8X4), scales=e_scales[n][:],
+                in_=e_grouped[n][:].rearrange("p i t -> p (i t)"),
+            )
+
+        def weigh_v(n):
+            o_acc[n] = psum.tile([P, NB, DH], F32, tag="sums", bufs=2, name="o_acc")
+            for i in range(NB):
+                nc.tensor.matmul_mx(
+                    out=o_acc[n][:, i, :],
+                    lhsT=e_codes[n][:, i * P:(i + 1) * P].bitcast(FP8X4),
+                    lhsT_scale=e_scales[n][:, i * P:(i + 1) * P],
+                    rhs=v_codes[:, n, :].bitcast(FP8X4),
+                    rhs_scale=v_scales[:, n, :],
+                    start=True, stop=True,
                 )
-                o_sb = soft.tile([P, NB, DH], F32, bufs=3)
-                nc.vector.tensor_tensor(
-                    out=o_sb[:], in0=o_acc[:],
-                    in1=factor[:].unsqueeze(2).to_broadcast([P, NB, DH]), op=ALU.mult,
-                )
-                nc.sync.dma_start(out=out_rows[:, :, h, :], in_=o_sb[:])
+
+        def finish(n):
+            b, h = divmod(n, H)
+            f, hf = divmod(h, HALF)
+            factor[n] = soft.tile([P, NB], F32, name="factor")
+            nc.vector.reciprocal(out=factor[n][:], in_=rowsum[n][:])
+            nc.vector.tensor_tensor(
+                out=factor[n][:], in0=factor[n][:], in1=row_on[b, f][:, :, hf], op=ALU.mult
+            )
+            o_sb = soft.tile([P, NB, DH], F32, bufs=3)
+            nc.vector.tensor_tensor(
+                out=o_sb[:], in0=o_acc[n][:],
+                in1=factor[n][:].unsqueeze(2).to_broadcast([P, NB, DH]), op=ALU.mult,
+            )
+            nc.sync.dma_start(
+                out=out[b].rearrange("(i p) (h d) -> p i h d", p=P, h=H)[:, :, h, :], in_=o_sb[:]
+            )
+
+        units = []
+        for b in range(B):
+            if b > 0:
+                for t in range(PACK):
+                    units.append(x_unit(b, t))
+            for quarter in range(PAIRS):
+                nb, pair = divmod(b * PAIRS + quarter + 1, PAIRS)
+                turns = []
+                if nb < B:
+                    turns = [turn_unit(k_nat, kT, nb, pair), turn_unit(q_nat, qT, nb, pair)]
+                if b == 0:
+                    units.append(turns[0])
+                    units.append(w_unit(2 * quarter))
+                    units.append(turns[1])
+                    units.append(w_unit(2 * quarter + 1))
+                else:
+                    units.extend(turns)
+                units.append(v_unit(b, 2 * quarter))
+                units.append(v_unit(b, 2 * quarter + 1))
+
+        first = [turn_unit(k_nat, kT, 0, 0), turn_unit(q_nat, qT, 0, 0)]
+        for t in range(PACK):
+            first.append(x_unit(0, t))
+        clear_signs(k_nat, 0, 0)
+        find_keys(0, 0)
+        make_addends(0)
+        make_addends(1)
+        for step in range(len(first) + 2):
+            for lag in range(3):
+                if 0 <= step - lag < len(first) and lag < len(first[step - lag]):
+                    first[step - lag][lag]()
+
+        searches = {
+            0: (find_keys, k_nat, 0, 1),
+            1: (find_queries, q_nat, 0, 0),
+            3: (find_queries, q_nat, 0, 1),
+            4: (find_keys, k_nat, 1, 0),
+            5: (find_queries, q_nat, 1, 0),
+            6: (find_keys, k_nat, 1, 1),
+            7: (find_queries, q_nat, 1, 1),
+        }
+        HEADS = B * H
+        TILES = HEADS * NB
+        weighed = 0
+        finished = 0
+        score(0, 0)
+        for step in range(TILES + 3 * NB):
+            n, i = divmod(step, NB)
+            if i == 0 and n + 2 < HEADS:
+                make_addends(n + 2)
+
+            for lag in (2, 1):
+                if 0 <= step - lag < len(units) and lag < len(units[step - lag]):
+                    units[step - lag][lag]()
+            if 1 <= n <= HEADS and i in (1, 3):
+                copy_e(n - 1, i // 2)
+            if 2 <= n <= HEADS + 1 and i == 0:
+                quantise_e(n - 2)
+            if finished < weighed:
+                finish(finished)
+                finished += 1
+
+            if step + 1 < TILES:
+                score((step + 1) // NB, (step + 1) % NB)
+            if step < len(units):
+                units[step][0]()
+            if (
+                weighed < HEADS and step >= (weighed + 2) * NB + 1
+                and (weighed // H, weighed % H) in v_ready
+            ):
+                weigh_v(weighed)
+                weighed += 1
+
+            if step < TILES:
+                negate(n, i)
+            if 1 <= step <= TILES:
+                exponent((step - 1) // NB, (step - 1) % NB)
+            if 1 <= n <= HEADS and i in (0, 2):
+                turn_e(n - 1, i // 2)
+            if n in searches and i in (1, 2):
+                find, nat, b, f = searches[n]
+                if i == 1:
+                    clear_signs(nat, b, f)
+                else:
+                    find(b, f)

@@ -99,37 +99,58 @@ def tile_multiheadattention_pa_kernel(tc, Q, K, x, Wv, mask, out):
 
         later = {}
         row_on = {}
-        unsigned = {}
 
-        def clear_signs(nat, b, f):
-            unsigned[b, f] = stage.tile([P, NB * HALF, DH // 2], I32, bufs=2, name="unsigned")
-            nc.vector.tensor_single_scalar(
-                out=unsigned[b, f][:],
-                in_=nat[b, f][:].bitcast(I32).rearrange("p c (h w) -> p (c h) w", h=HALF),
-                scalar=NO_SIGN_BITS, op=ALU.bitwise_and,
-            )
+        def search(nat, b, f):
+            words = nat[b, f][:].bitcast(I32).rearrange("p c (h w) -> p (c h) w", h=HALF)
+            rows = NB * HALF
+            held = {}
 
-        def find_keys(b, f):
-            bits = stage.tile([P, NB * HALF], F32, bufs=2)
-            nc.vector.tensor_reduce(out=bits[:], in_=unsigned[b, f][:], axis=AX.X, op=ALU.max)
-            later[b, f] = keep.tile([P, NB, HALF], F32, name="later%d%d" % (b, f))
-            nc.vector.tensor_scalar(
-                out=later[b, f][:].rearrange("p c h -> p (c h)"), in0=bits[:],
-                scalar1=0.0, scalar2=ABSENT_KEY, op0=ALU.is_equal, op1=ALU.mult,
-            )
+            def join(level):
+                src = held["words"][:] if level else words
+                width = DH // 4 >> level
+                held["words"] = stage.tile(
+                    [P, rows, width], I32, bufs=2, name="joined%d" % level
+                )
+                nc.vector.tensor_tensor(
+                    out=held["words"][:], in0=src[:, :, 0:width], in1=src[:, :, width:2 * width],
+                    op=ALU.bitwise_or,
+                )
 
-        def find_queries(b, f):
-            bits = stage.tile([P, NB * HALF], F32, bufs=2)
-            nc.vector.tensor_reduce(out=bits[:], in_=unsigned[b, f][:], axis=AX.X, op=ALU.max)
-            row_on[b, f] = keep.tile([P, NB, HALF], F32, name="row_on%d%d" % (b, f))
-            nc.vector.tensor_single_scalar(
-                out=row_on[b, f][:].rearrange("p c h -> p (c h)"), in_=bits[:],
-                scalar=0.0, op=ALU.is_gt,
-            )
-            nc.vector.tensor_tensor(
-                out=row_on[b, f][:], in0=row_on[b, f][:],
-                in1=mask_sb[:, b, :].unsqueeze(2).to_broadcast([P, NB, HALF]), op=ALU.mult,
-            )
+            def clear_signs():
+                held["magnitudes"] = stage.tile([P, rows, DH // 8], I32, bufs=2, name="magnitudes")
+                nc.vector.tensor_single_scalar(
+                    out=held["magnitudes"][:], in_=held["words"][:], scalar=NO_SIGN_BITS,
+                    op=ALU.bitwise_and,
+                )
+
+            def largest():
+                held["bits"] = stage.tile([P, rows], F32, bufs=2, name="bits")
+                nc.vector.tensor_reduce(
+                    out=held["bits"][:], in_=held["magnitudes"][:], axis=AX.X, op=ALU.max
+                )
+
+            def key_addend():
+                later[b, f] = keep.tile([P, NB, HALF], F32, name="later%d%d" % (b, f))
+                nc.vector.tensor_scalar(
+                    out=later[b, f][:].rearrange("p c h -> p (c h)"), in0=held["bits"][:],
+                    scalar1=0.0, scalar2=ABSENT_KEY, op0=ALU.is_equal, op1=ALU.mult,
+                )
+
+            def query_sign():
+                row_on[b, f] = keep.tile([P, NB, HALF], F32, name="row_on%d%d" % (b, f))
+                nc.vector.tensor_single_scalar(
+                    out=row_on[b, f][:].rearrange("p c h -> p (c h)"), in_=held["bits"][:],
+                    scalar=0.0, op=ALU.is_gt,
+                )
+
+            def query_mask():
+                nc.vector.tensor_tensor(
+                    out=row_on[b, f][:], in0=row_on[b, f][:],
+                    in1=mask_sb[:, b, :].unsqueeze(2).to_broadcast([P, NB, HALF]), op=ALU.mult,
+                )
+
+            found = [key_addend] if nat is k_nat else [query_sign, query_mask]
+            return [lambda: join(0), lambda: join(1), clear_signs, largest] + found
 
         kT = {}
         qT = {}
@@ -330,14 +351,19 @@ def tile_multiheadattention_pa_kernel(tc, Q, K, x, Wv, mask, out):
                     start=True, stop=True,
                 )
 
-        def finish(n):
+        def invert(n):
+            factor[n] = soft.tile([P, NB], F32, bufs=4, name="factor")
+            nc.vector.reciprocal(out=factor[n][:], in_=rowsum[n][:])
+
+        def weigh_rows(n):
             b, h = divmod(n, H)
             f, hf = divmod(h, HALF)
-            factor[n] = soft.tile([P, NB], F32, name="factor")
-            nc.vector.reciprocal(out=factor[n][:], in_=rowsum[n][:])
             nc.vector.tensor_tensor(
                 out=factor[n][:], in0=factor[n][:], in1=row_on[b, f][:, :, hf], op=ALU.mult
             )
+
+        def finish(n):
+            b, h = divmod(n, H)
             o_sb = soft.tile([P, NB, DH], F32, bufs=3)
             nc.vector.tensor_tensor(
                 out=o_sb[:], in0=o_acc[n][:],
@@ -347,47 +373,33 @@ def tile_multiheadattention_pa_kernel(tc, Q, K, x, Wv, mask, out):
                 out=out[b].rearrange("(i p) (h d) -> p i h d", p=P, h=H)[:, :, h, :], in_=o_sb[:]
             )
 
-        units = []
-        for b in range(B):
-            if b > 0:
-                for t in range(PACK):
-                    units.append(x_unit(b, t))
-            for quarter in range(PAIRS):
-                nb, pair = divmod(b * PAIRS + quarter + 1, PAIRS)
-                turns = []
-                if nb < B:
-                    turns = [turn_unit(k_nat, kT, nb, pair), turn_unit(q_nat, qT, nb, pair)]
-                if b == 0:
-                    units.append(turns[0])
-                    units.append(w_unit(2 * quarter))
-                    units.append(turns[1])
-                    units.append(w_unit(2 * quarter + 1))
-                else:
-                    units.extend(turns)
-                units.append(v_unit(b, 2 * quarter))
-                units.append(v_unit(b, 2 * quarter + 1))
-
-        first = [turn_unit(k_nat, kT, 0, 0), turn_unit(q_nat, qT, 0, 0)]
+        units = {}
+        for pair in range(1, B * PAIRS):
+            units[NB * (2 * pair - 2)] = turn_unit(k_nat, kT, pair // PAIRS, pair % PAIRS)
+            units[NB * (2 * pair - 1)] = turn_unit(q_nat, qT, pair // PAIRS, pair % PAIRS)
+        for h in range(H):
+            units[NB * (h + 1) + 2] = w_unit(h)
+            units[NB * (h + 2) + 1] = v_unit(0, h)
+            units[NB * (H + 2 + h // 2) + 1 + 2 * (h % 2)] = v_unit(1, h)
         for t in range(PACK):
-            first.append(x_unit(0, t))
-        clear_signs(k_nat, 0, 0)
-        find_keys(0, 0)
-        make_addends(0)
-        make_addends(1)
-        for step in range(len(first) + 2):
-            for lag in range(3):
-                if 0 <= step - lag < len(first) and lag < len(first[step - lag]):
-                    first[step - lag][lag]()
+            units[NB * (t // 3) + 1 + t % 3] = x_unit(0, t)
+            units[NB * (H - 3 + t) + 3] = x_unit(1, t)
 
-        searches = {
-            0: (find_keys, k_nat, 0, 1),
-            1: (find_queries, q_nat, 0, 0),
-            3: (find_queries, q_nat, 0, 1),
-            4: (find_keys, k_nat, 1, 0),
-            5: (find_queries, q_nat, 1, 0),
-            6: (find_keys, k_nat, 1, 1),
-            7: (find_queries, q_nat, 1, 1),
-        }
+        searches = [search(k_nat, 0, 0)]
+        for run in searches[0]:
+            run()
+        make_addends(0)
+        for stages in [turn_unit(k_nat, kT, 0, 0), turn_unit(q_nat, qT, 0, 0)]:
+            for run in stages:
+                run()
+
+        search_steps = []
+        for nat, b, f in (
+            (q_nat, 0, 0), (k_nat, 0, 1), (q_nat, 0, 1),
+            (k_nat, 1, 0), (q_nat, 1, 0), (k_nat, 1, 1), (q_nat, 1, 1),
+        ):
+            search_steps.extend(search(nat, b, f))
+
         HEADS = B * H
         TILES = HEADS * NB
         weighed = 0
@@ -395,11 +407,12 @@ def tile_multiheadattention_pa_kernel(tc, Q, K, x, Wv, mask, out):
         score(0, 0)
         for step in range(TILES + 3 * NB):
             n, i = divmod(step, NB)
-            if i == 0 and n + 2 < HEADS:
-                make_addends(n + 2)
+            if i == 0 and n + 1 < HEADS:
+                make_addends(n + 1)
 
+            ready = (weighed // H, weighed % H) in v_ready
             for lag in (2, 1):
-                if 0 <= step - lag < len(units) and lag < len(units[step - lag]):
+                if step - lag in units and lag < len(units[step - lag]):
                     units[step - lag][lag]()
             if 1 <= n <= HEADS and i in (1, 3):
                 copy_e(n - 1, i // 2)
@@ -411,12 +424,9 @@ def tile_multiheadattention_pa_kernel(tc, Q, K, x, Wv, mask, out):
 
             if step + 1 < TILES:
                 score((step + 1) // NB, (step + 1) % NB)
-            if step < len(units):
+            if step in units:
                 units[step][0]()
-            if (
-                weighed < HEADS and step >= (weighed + 2) * NB + 1
-                and (weighed // H, weighed % H) in v_ready
-            ):
+            if weighed < HEADS and step >= (weighed + 2) * NB + 1 and i % 2 == 1 and ready:
                 weigh_v(weighed)
                 weighed += 1
 
@@ -426,9 +436,9 @@ def tile_multiheadattention_pa_kernel(tc, Q, K, x, Wv, mask, out):
                 exponent((step - 1) // NB, (step - 1) % NB)
             if 1 <= n <= HEADS and i in (0, 2):
                 turn_e(n - 1, i // 2)
-            if n in searches and i in (1, 2):
-                find, nat, b, f = searches[n]
-                if i == 1:
-                    clear_signs(nat, b, f)
-                else:
-                    find(b, f)
+            if step < len(search_steps):
+                search_steps[step]()
+            if 1 <= n <= HEADS and i == 2:
+                invert(n - 1)
+            if 1 <= n <= HEADS and i == 3:
+                weigh_rows(n - 1)

@@ -267,17 +267,17 @@ def tile_multiheadattention_pa_kernel(tc, Q, K, x, Wv, mask, out):
         scores = {}
         o_acc = {}
 
-        def make_addends(n):
+        def make_addends(n, j):
             b, h = divmod(n, H)
             f, hf = divmod(h, HALF)
-            addends[n] = soft.tile([P, NB, 3, P], F32, bufs=3, name="addends")
-            for j in range(NB):
-                kinds = slice(1 if j == NB - 1 else 0, 2 if j == 0 else 3)
-                nc.gpsimd.tensor_scalar(
-                    out=addends[n][:, j, kinds, :], in0=causal[:, kinds, :],
-                    scalar1=1.0, scalar2=later[b, f][:, j, hf:hf + 1],
-                    op0=ALU.mult, op1=ALU.add,
-                )
+            if j == 0:
+                addends[n] = soft.tile([P, NB, 3, P], F32, bufs=3, name="addends")
+            kinds = slice(1 if j == NB - 1 else 0, 2 if j == 0 else 3)
+            nc.gpsimd.tensor_scalar(
+                out=addends[n][:, j, kinds, :], in0=causal[:, kinds, :],
+                scalar1=1.0, scalar2=later[b, f][:, j, hf:hf + 1],
+                op0=ALU.mult, op1=ALU.add,
+            )
 
         def score(n, i):
             b, h = divmod(n, H)
@@ -312,38 +312,40 @@ def tile_multiheadattention_pa_kernel(tc, Q, K, x, Wv, mask, out):
                 bias=shift[n][:, i:i + 1], scale=-1.0, accum_out=rowsum[n][:, i:i + 1],
             )
 
-        def turn_e(n, half):
+        def turn_e(n, lo, hi):
             words = e_sb[n][:].bitcast(F32)
-            e_turned[n, half] = psum.tile([P, 2, 2 * P], F32, tag="turned", bufs=3, name="turned")
+            e_turned[n, lo] = psum.tile([P, 2, (hi - lo) * P], F32, tag="turned", bufs=3, name="turned")
             for u in range(2):
-                for ii in range(2):
+                for i in range(lo, hi):
                     nc.tensor.transpose(
-                        out=e_turned[n, half][:, u, ii * P:(ii + 1) * P],
-                        in_=words[:, 2 * half + ii, u * P:(u + 1) * P],
-                        identity=ident_f32[:],
+                        out=e_turned[n, lo][:, u, (i - lo) * P:(i - lo + 1) * P],
+                        in_=words[:, i, u * P:(u + 1) * P], identity=ident_f32[:],
                     )
 
-        def copy_e(n, half):
-            if half == 0:
-                e_grouped[n] = soft.tile([P, NB * P, PACK], BF16, align_bytes=64, bufs=3, name="e_grouped")
+        def copy_e(n, lo, hi):
+            if lo == 0:
+                e_grouped[n] = soft.tile(
+                    [P, NB * P, PACK], BF16, align_bytes=64, bufs=3, name="e_grouped"
+                )
             nc.scalar.copy(
-                out=e_grouped[n][:, half * 2 * P:(half + 1) * 2 * P, :].bitcast(F32),
-                in_=e_turned[n, half][:].rearrange("p u i -> p i u"),
+                out=e_grouped[n][:, lo * P:hi * P, :].bitcast(F32),
+                in_=e_turned[n, lo][:].rearrange("p u i -> p i u"),
             )
 
-        def quantise_e(n):
-            e_codes[n] = soft.tile([P, NB * P], U32, align_bytes=64, bufs=4, name="e_codes")
-            e_scales[n] = soft.tile([P, NB * P], U8, align_bytes=64, bufs=4, name="e_scales")
+        def quantise_e(n, lo, hi):
+            if lo == 0:
+                e_codes[n] = soft.tile([P, NB * P], U32, align_bytes=64, bufs=4, name="e_codes")
+                e_scales[n] = soft.tile([P, NB * P], U8, align_bytes=64, bufs=4, name="e_scales")
             nc.vector.quantize_mx(
-                out=e_codes[n][:].bitcast(FP8X4), scales=e_scales[n][:],
-                in_=e_grouped[n][:].rearrange("p i t -> p (i t)"),
+                out=e_codes[n][:, lo * P:hi * P].bitcast(FP8X4), scales=e_scales[n][:, lo * P:hi * P],
+                in_=e_grouped[n][:, lo * P:hi * P, :].rearrange("p i t -> p (i t)"),
             )
 
-        def weigh_v(n):
-            o_acc[n] = psum.tile([P, NB, DH], F32, tag="sums", bufs=2, name="o_acc")
-            for i in range(NB):
+        def weigh_v(n, lo, hi):
+            o_acc[n, lo] = psum.tile([P, hi - lo, DH], F32, tag="sums", bufs=2, name="o_acc")
+            for i in range(lo, hi):
                 nc.tensor.matmul_mx(
-                    out=o_acc[n][:, i, :],
+                    out=o_acc[n, lo][:, i - lo, :],
                     lhsT=e_codes[n][:, i * P:(i + 1) * P].bitcast(FP8X4),
                     lhsT_scale=e_scales[n][:, i * P:(i + 1) * P],
                     rhs=v_codes[:, n, :].bitcast(FP8X4),
@@ -351,26 +353,28 @@ def tile_multiheadattention_pa_kernel(tc, Q, K, x, Wv, mask, out):
                     start=True, stop=True,
                 )
 
-        def invert(n):
-            factor[n] = soft.tile([P, NB], F32, bufs=4, name="factor")
-            nc.vector.reciprocal(out=factor[n][:], in_=rowsum[n][:])
+        def invert(n, lo, hi):
+            if lo == 0:
+                factor[n] = soft.tile([P, NB], F32, bufs=4, name="factor")
+            nc.vector.reciprocal(out=factor[n][:, lo:hi], in_=rowsum[n][:, lo:hi])
 
-        def weigh_rows(n):
+        def weigh_rows(n, lo, hi):
             b, h = divmod(n, H)
             f, hf = divmod(h, HALF)
-            nc.vector.tensor_tensor(
-                out=factor[n][:], in0=factor[n][:], in1=row_on[b, f][:, :, hf], op=ALU.mult
+            nc.gpsimd.tensor_tensor(
+                out=factor[n][:, lo:hi], in0=factor[n][:, lo:hi], in1=row_on[b, f][:, lo:hi, hf],
+                op=ALU.mult,
             )
 
-        def finish(n):
+        def finish(n, lo, hi):
             b, h = divmod(n, H)
-            o_sb = soft.tile([P, NB, DH], F32, bufs=3)
+            o_sb = soft.tile([P, hi - lo, DH], F32, bufs=6)
             nc.vector.tensor_tensor(
-                out=o_sb[:], in0=o_acc[n][:],
-                in1=factor[n][:].unsqueeze(2).to_broadcast([P, NB, DH]), op=ALU.mult,
+                out=o_sb[:], in0=o_acc[n, lo][:],
+                in1=factor[n][:, lo:hi].unsqueeze(2).to_broadcast([P, hi - lo, DH]), op=ALU.mult,
             )
             nc.sync.dma_start(
-                out=out[b].rearrange("(i p) (h d) -> p i h d", p=P, h=H)[:, :, h, :], in_=o_sb[:]
+                out=out[b].rearrange("(i p) (h d) -> p i h d", p=P, h=H)[:, lo:hi, h, :], in_=o_sb[:]
             )
 
         units = {}
@@ -388,7 +392,8 @@ def tile_multiheadattention_pa_kernel(tc, Q, K, x, Wv, mask, out):
         searches = [search(k_nat, 0, 0)]
         for run in searches[0]:
             run()
-        make_addends(0)
+        for j in range(NB):
+            make_addends(0, j)
         for stages in [turn_unit(k_nat, kT, 0, 0), turn_unit(q_nat, qT, 0, 0)]:
             for run in stages:
                 run()
@@ -405,40 +410,67 @@ def tile_multiheadattention_pa_kernel(tc, Q, K, x, Wv, mask, out):
         weighed = 0
         finished = 0
         score(0, 0)
-        for step in range(TILES + 3 * NB):
+        for step in range(TILES):
             n, i = divmod(step, NB)
-            if i == 0 and n + 1 < HEADS:
-                make_addends(n + 1)
+            if n + 1 < HEADS and i == 0:
+                for j in range(NB):
+                    make_addends(n + 1, j)
 
             ready = (weighed // H, weighed % H) in v_ready
             for lag in (2, 1):
                 if step - lag in units and lag < len(units[step - lag]):
                     units[step - lag][lag]()
-            if 1 <= n <= HEADS and i in (1, 3):
-                copy_e(n - 1, i // 2)
-            if 2 <= n <= HEADS + 1 and i == 0:
-                quantise_e(n - 2)
+            if n >= 1 and i % 2 == 1:
+                copy_e(n - 1, i - 1, i + 1)
+            if n >= 2 and i == 0:
+                quantise_e(n - 2, 0, NB)
             if finished < weighed:
-                finish(finished)
+                finish(finished, 0, NB)
                 finished += 1
 
             if step + 1 < TILES:
                 score((step + 1) // NB, (step + 1) % NB)
             if step in units:
                 units[step][0]()
-            if weighed < HEADS and step >= (weighed + 2) * NB + 1 and i % 2 == 1 and ready:
-                weigh_v(weighed)
+            if weighed < n - 1 and i % 2 == 1 and ready:
+                weigh_v(weighed, 0, NB)
                 weighed += 1
 
-            if step < TILES:
-                negate(n, i)
-            if 1 <= step <= TILES:
+            negate(n, i)
+            if step >= 1:
                 exponent((step - 1) // NB, (step - 1) % NB)
-            if 1 <= n <= HEADS and i in (0, 2):
-                turn_e(n - 1, i // 2)
+            if n >= 1 and i % 2 == 0:
+                turn_e(n - 1, i, i + 2)
             if step < len(search_steps):
                 search_steps[step]()
-            if 1 <= n <= HEADS and i == 2:
-                invert(n - 1)
-            if 1 <= n <= HEADS and i == 3:
-                weigh_rows(n - 1)
+            if n >= 1 and i == 2:
+                invert(n - 1, 0, NB)
+            if n >= 1 and i == 3:
+                weigh_rows(n - 1, 0, NB)
+
+        last = HEADS - 1
+        parts = [(0, 2), (2, 3), (3, 4)]
+        turn_e(last, *parts[0])
+        exponent(last, NB - 1)
+        quantise_e(last - 1, 0, NB)
+        if finished < weighed:
+            finish(finished, 0, NB)
+            finished += 1
+        copy_e(last, *parts[0])
+        turn_e(last, *parts[1])
+        copy_e(last, *parts[1])
+        weigh_v(last - 1, 0, NB)
+        turn_e(last, *parts[2])
+        copy_e(last, *parts[2])
+        quantise_e(last, *parts[0])
+        invert(last, 0, NB)
+        quantise_e(last, *parts[1])
+        finish(last - 1, 0, NB)
+        weigh_rows(last, 0, NB)
+        weigh_v(last, *parts[0])
+        quantise_e(last, *parts[2])
+        finish(last, *parts[0])
+        weigh_v(last, *parts[1])
+        weigh_v(last, *parts[2])
+        finish(last, *parts[1])
+        finish(last, *parts[2])

@@ -41,9 +41,9 @@ def tile_multiheadattention_pa_kernel(tc, Q, K, x, Wv, mask, out):
         soft = ctx.enter_context(tc.tile_pool(name="soft", bufs=2))
         psum = ctx.enter_context(tc.psum_pool(name="psum", bufs=2))
 
-        ident_bf = keep.tile([P, P], BF16)
+        ident_bf = keep.tile([P, P], BF16, align_bytes=256)
         make_identity(nc, ident_bf[:])
-        ident_f32 = keep.tile([P, P], F32)
+        ident_f32 = keep.tile([P, P], F32, align_bytes=256)
         make_identity(nc, ident_f32[:])
         causal = keep.tile([P, 3, P], F32)
         nc.gpsimd.memset(causal[:, 0:2, :], EARLIER_KEY)
@@ -60,12 +60,12 @@ def tile_multiheadattention_pa_kernel(tc, Q, K, x, Wv, mask, out):
         x_nat = {}
         w_nat = {}
         for b in range(B):
-            x_nat[b] = keep.tile([P, 2, 2 * D], BF16, name="x_nat%d" % b)
+            x_nat[b] = keep.tile([P, 2, 2 * D], BF16, align_bytes=256, name="x_nat%d" % b)
             for f in range(2):
-                k_nat[b, f] = keep.tile([P, NB, D // 2], BF16, name="k_nat%d%d" % (b, f))
-                q_nat[b, f] = keep.tile([P, NB, D // 2], BF16, name="q_nat%d%d" % (b, f))
+                k_nat[b, f] = keep.tile([P, NB, D // 2], BF16, align_bytes=256, name="k_nat%d%d" % (b, f))
+                q_nat[b, f] = keep.tile([P, NB, D // 2], BF16, align_bytes=256, name="q_nat%d%d" % (b, f))
         for f in range(2):
-            w_nat[f] = keep.tile([P, HALF, D], BF16, name="w_nat%d" % f)
+            w_nat[f] = keep.tile([P, HALF, D], BF16, align_bytes=256, name="w_nat%d" % f)
         mask_sb = keep.tile([P, B, NB], BF16)
 
         def load_heads(b, f):
@@ -157,12 +157,12 @@ def tile_multiheadattention_pa_kernel(tc, Q, K, x, Wv, mask, out):
         x_codes = {}
         x_scales = {}
         for b in range(B):
-            x_codes[b] = keep.tile([P, PACK, G * P], U32, align_bytes=64, name="x_codes%d" % b)
-            x_scales[b] = keep.tile([P, PACK, G * P], U8, align_bytes=64, name="x_scales%d" % b)
-        w_codes = keep.tile([P, H, G * P], U32, align_bytes=64)
-        w_scales = keep.tile([P, H, G * P], U8, align_bytes=64)
-        v_codes = keep.tile([P, B * H, DH], U32, align_bytes=64)
-        v_scales = keep.tile([P, B * H, DH], U8, align_bytes=64)
+            x_codes[b] = keep.tile([P, PACK, G * P], U32, align_bytes=256, name="x_codes%d" % b)
+            x_scales[b] = keep.tile([P, PACK, G * P], U8, align_bytes=256, name="x_scales%d" % b)
+        w_codes = keep.tile([P, H, G * P], U32, align_bytes=256)
+        w_scales = keep.tile([P, H, G * P], U8, align_bytes=256)
+        v_codes = keep.tile([P, B * H, DH], U32, align_bytes=256)
+        v_scales = keep.tile([P, B * H, DH], U8, align_bytes=256)
 
         def turn_unit(nat, turned_sb, b, pair):
             f, first = divmod(2 * pair, HALF)
@@ -180,7 +180,7 @@ def tile_multiheadattention_pa_kernel(tc, Q, K, x, Wv, mask, out):
 
             def copy():
                 which = "kT" if nat is k_nat else "qT"
-                turned_sb[b, pair] = keep.tile([P, 2, T], BF16, name="%s%d%d" % (which, b, pair))
+                turned_sb[b, pair] = keep.tile([P, 2, T], BF16, align_bytes=256, name="%s%d%d" % (which, b, pair))
                 nc.scalar.copy(out=turned_sb[b, pair][:], in_=held["psum"][:])
 
             return [fill, copy]
@@ -197,7 +197,7 @@ def tile_multiheadattention_pa_kernel(tc, Q, K, x, Wv, mask, out):
                     )
 
             def copy():
-                held["sb"] = stage.tile([P, G, P, PACK], BF16, align_bytes=64, name="grouped")
+                held["sb"] = stage.tile([P, G, P, PACK], BF16, align_bytes=256, name="grouped")
                 nc.scalar.copy(
                     out=held["sb"][:].bitcast(F32),
                     in_=held["psum"][:].rearrange("p (g u) r -> p g r u", g=G),
@@ -240,7 +240,7 @@ def tile_multiheadattention_pa_kernel(tc, Q, K, x, Wv, mask, out):
                         )
 
             def copy():
-                held["sb"] = stage.tile([P, DH, PACK], BF16, align_bytes=64, name="v_grouped")
+                held["sb"] = stage.tile([P, DH, PACK], BF16, align_bytes=256, name="v_grouped")
                 nc.scalar.copy(
                     out=held["sb"][:], in_=held["psum"][:].rearrange("p t d -> p d t")
                 )
@@ -271,7 +271,7 @@ def tile_multiheadattention_pa_kernel(tc, Q, K, x, Wv, mask, out):
             b, h = divmod(n, H)
             f, hf = divmod(h, HALF)
             if j == 0:
-                addends[n] = soft.tile([P, NB, 3, P], F32, bufs=3, name="addends")
+                addends[n] = soft.tile([P, NB, 3, P], F32, bufs=3, align_bytes=256, name="addends")
             kinds = slice(1 if j == NB - 1 else 0, 2 if j == 0 else 3)
             nc.gpsimd.tensor_scalar(
                 out=addends[n][:, j, kinds, :], in0=causal[:, kinds, :],
@@ -305,7 +305,7 @@ def tile_multiheadattention_pa_kernel(tc, Q, K, x, Wv, mask, out):
 
         def exponent(n, i):
             if i == 0:
-                e_sb[n] = soft.tile([P, NB, T], BF16, bufs=3, name="e_sb")
+                e_sb[n] = soft.tile([P, NB, T], BF16, bufs=3, align_bytes=256, name="e_sb")
                 rowsum[n] = soft.tile([P, NB], F32, bufs=4, name="rowsum")
             nc.scalar.activation(
                 out=e_sb[n][:, i, :], in_=negated[n, i][:], func=ACT.Exp,
@@ -325,7 +325,7 @@ def tile_multiheadattention_pa_kernel(tc, Q, K, x, Wv, mask, out):
         def copy_e(n, lo, hi):
             if lo == 0:
                 e_grouped[n] = soft.tile(
-                    [P, NB * P, PACK], BF16, align_bytes=64, bufs=3, name="e_grouped"
+                    [P, NB * P, PACK], BF16, align_bytes=256, bufs=3, name="e_grouped"
                 )
             nc.scalar.copy(
                 out=e_grouped[n][:, lo * P:hi * P, :].bitcast(F32),
@@ -334,8 +334,8 @@ def tile_multiheadattention_pa_kernel(tc, Q, K, x, Wv, mask, out):
 
         def quantise_e(n, lo, hi):
             if lo == 0:
-                e_codes[n] = soft.tile([P, NB * P], U32, align_bytes=64, bufs=4, name="e_codes")
-                e_scales[n] = soft.tile([P, NB * P], U8, align_bytes=64, bufs=4, name="e_scales")
+                e_codes[n] = soft.tile([P, NB * P], U32, align_bytes=256, bufs=4, name="e_codes")
+                e_scales[n] = soft.tile([P, NB * P], U8, align_bytes=256, bufs=4, name="e_scales")
             nc.vector.quantize_mx(
                 out=e_codes[n][:, lo * P:hi * P].bitcast(FP8X4), scales=e_scales[n][:, lo * P:hi * P],
                 in_=e_grouped[n][:, lo * P:hi * P, :].rearrange("p i t -> p (i t)"),
@@ -384,7 +384,10 @@ def tile_multiheadattention_pa_kernel(tc, Q, K, x, Wv, mask, out):
         for h in range(H):
             units[NB * (h + 1) + 2] = w_unit(h)
             units[NB * (h + 2) + 1] = v_unit(0, h)
-            units[NB * (H + 2 + h // 2) + 1 + 2 * (h % 2)] = v_unit(1, h)
+            if h < 4:
+                units[NB * (H + 2 + h // 2) + 1 + 2 * (h % 2)] = v_unit(1, h)
+            else:
+                units[NB * (H + h) + 1] = v_unit(1, h)
         for t in range(PACK):
             units[NB * (t // 3) + 1 + t % 3] = x_unit(0, t)
             units[NB * (H - 3 + t) + 3] = x_unit(1, t)

@@ -45,14 +45,12 @@ def tile_multiheadattention_pa_kernel(tc, Q, K, x, Wv, mask, out):
         make_identity(nc, ident_bf[:])
         ident_f32 = keep.tile([P, P], F32, align_bytes=256)
         make_identity(nc, ident_f32[:])
-        causal = keep.tile([P, 3, P], F32)
-        nc.gpsimd.memset(causal[:, 0:2, :], EARLIER_KEY)
-        nc.gpsimd.memset(causal[:, 2, :], 0.0)
+        causal = keep.tile([P, P], F32)
+        nc.gpsimd.memset(causal[:], EARLIER_KEY)
         nc.gpsimd.affine_select(
-            out=causal[:, 1, :], in_=causal[:, 1, :], pattern=[[1, P]], compare_op=ALU.is_ge,
+            out=causal[:], in_=causal[:], pattern=[[1, P]], compare_op=ALU.is_ge,
             fill=0.0, base=0, channel_multiplier=-1,
         )
-
         ctx.enter_context(tc.manual_schedule())
 
         k_nat = {}
@@ -98,6 +96,7 @@ def tile_multiheadattention_pa_kernel(tc, Q, K, x, Wv, mask, out):
         load_heads(1, 1)
 
         later = {}
+        earlier = {}
         row_on = {}
 
         def search(nat, b, f):
@@ -136,6 +135,12 @@ def tile_multiheadattention_pa_kernel(tc, Q, K, x, Wv, mask, out):
                     scalar1=0.0, scalar2=ABSENT_KEY, op0=ALU.is_equal, op1=ALU.mult,
                 )
 
+            def earlier_addend():
+                earlier[b, f] = keep.tile([P, NB, HALF], F32, name="earlier%d%d" % (b, f))
+                nc.vector.tensor_scalar_add(
+                    out=earlier[b, f][:], in0=later[b, f][:], scalar1=EARLIER_KEY
+                )
+
             def query_sign():
                 row_on[b, f] = keep.tile([P, NB, HALF], F32, name="row_on%d%d" % (b, f))
                 nc.vector.tensor_single_scalar(
@@ -149,7 +154,7 @@ def tile_multiheadattention_pa_kernel(tc, Q, K, x, Wv, mask, out):
                     in1=mask_sb[:, b, :].unsqueeze(2).to_broadcast([P, NB, HALF]), op=ALU.mult,
                 )
 
-            found = [key_addend] if nat is k_nat else [query_sign, query_mask]
+            found = [key_addend, earlier_addend] if nat is k_nat else [query_sign, query_mask]
             return [lambda: join(0), lambda: join(1), clear_signs, largest] + found
 
         kT = {}
@@ -271,16 +276,16 @@ def tile_multiheadattention_pa_kernel(tc, Q, K, x, Wv, mask, out):
             b, h = divmod(n, H)
             f, hf = divmod(h, HALF)
             if j == 0:
-                addends[n] = soft.tile([P, NB, 3, P], F32, bufs=3, align_bytes=256, name="addends")
-            kinds = slice(1 if j == NB - 1 else 0, 2 if j == 0 else 3)
+                addends[n] = soft.tile([P, NB, P], F32, bufs=3, name="addends")
             nc.gpsimd.tensor_scalar(
-                out=addends[n][:, j, kinds, :], in0=causal[:, kinds, :],
+                out=addends[n][:, j, :], in0=causal[:],
                 scalar1=1.0, scalar2=later[b, f][:, j, hf:hf + 1],
                 op0=ALU.mult, op1=ALU.add,
             )
 
         def score(n, i):
             b, h = divmod(n, H)
+            f, hf = divmod(h, HALF)
             pair, hh = divmod(h, 2)
             scores[n, i] = psum.tile([P, T], F32, tag="scores", bufs=3, name="scores")
             nc.tensor.matmul(
@@ -288,9 +293,13 @@ def tile_multiheadattention_pa_kernel(tc, Q, K, x, Wv, mask, out):
                 rhs=kT[b, pair][:, hh, :], start=True, stop=False,
             )
             for j in range(NB):
-                kind = 0 if j < i else 1 if j == i else 2
+                if j == i:
+                    addend = addends[n][:, j, :]
+                else:
+                    one_a_key = earlier if j < i else later
+                    addend = one_a_key[b, f][:, j, hf:hf + 1].to_broadcast([P, P])
                 nc.tensor.matmul(
-                    out=scores[n, i][:, j * P:(j + 1) * P], lhsT=addends[n][:, j, kind, :],
+                    out=scores[n, i][:, j * P:(j + 1) * P], lhsT=addend,
                     rhs=ident_f32[:], is_transpose=True, start=False, stop=(j == NB - 1),
                 )
 

@@ -21,7 +21,7 @@ NB = T // P
 PACK = 4
 K_PASS = P * PACK
 G = D // K_PASS
-HALF = H // 2
+LOADS = (((0, 2), (2, 2), (4, 4)), ((0, 4), (4, 4)))
 PAIRS = H // 2
 
 SCALE = 1.0 / math.sqrt(DH)
@@ -51,6 +51,9 @@ def tile_multiheadattention_pa_kernel(tc, Q, K, x, Wv, mask, out):
             out=causal[:], in_=causal[:], pattern=[[1, P]], compare_op=ALU.is_ge,
             fill=0.0, base=0, channel_multiplier=-1,
         )
+        ones = keep.tile([P, T], BF16)
+        nc.vector.memset(ones[:], 1.0)
+
         ctx.enter_context(tc.manual_schedule())
 
         k_nat = {}
@@ -59,15 +62,28 @@ def tile_multiheadattention_pa_kernel(tc, Q, K, x, Wv, mask, out):
         w_nat = {}
         for b in range(B):
             x_nat[b] = keep.tile([P, 2, 2 * D], BF16, align_bytes=256, name="x_nat%d" % b)
-            for f in range(2):
-                k_nat[b, f] = keep.tile([P, NB, D // 2], BF16, align_bytes=256, name="k_nat%d%d" % (b, f))
-                q_nat[b, f] = keep.tile([P, NB, D // 2], BF16, align_bytes=256, name="q_nat%d%d" % (b, f))
+            for f in range(len(LOADS[b])):
+                cols = LOADS[b][f][1] * DH
+                k_nat[b, f] = keep.tile(
+                    [P, NB, cols], BF16, align_bytes=256, name="k_nat%d%d" % (b, f)
+                )
+                q_nat[b, f] = keep.tile(
+                    [P, NB, cols], BF16, align_bytes=256, name="q_nat%d%d" % (b, f)
+                )
         for f in range(2):
-            w_nat[f] = keep.tile([P, HALF, D], BF16, align_bytes=256, name="w_nat%d" % f)
-        mask_sb = keep.tile([P, B, NB], BF16)
+            w_nat[f] = keep.tile([P, H // 2, D], BF16, align_bytes=256, name="w_nat%d" % f)
+        mask_rows = keep.tile([P, P], BF16)
+        mask_sb = keep.tile([P, B, NB], F32)
+        nc.vector.memset(mask_rows[:], 0.0)
+
+        def load_of(b, h):
+            for f, (first, heads) in enumerate(LOADS[b]):
+                if first <= h < first + heads:
+                    return f, h - first
 
         def load_heads(b, f):
-            cols = slice(f * D // 2, (f + 1) * D // 2)
+            first, heads = LOADS[b][f]
+            cols = slice(first * DH, (first + heads) * DH)
             for nat, src in ((k_nat, K), (q_nat, Q)):
                 nc.sync.dma_start(
                     out=nat[b, f][:], in_=src[b].rearrange("(c p) d -> p c d", p=P)[:, :, cols]
@@ -81,15 +97,17 @@ def tile_multiheadattention_pa_kernel(tc, Q, K, x, Wv, mask, out):
         def load_w(f):
             nc.sync.dma_start(
                 out=w_nat[f][:],
-                in_=Wv.rearrange("(r p) k -> p r k", p=P)[:, f * HALF:(f + 1) * HALF, :],
+                in_=Wv.rearrange("(r p) k -> p r k", p=P)[:, f * H // 2:(f + 1) * H // 2, :],
             )
 
         load_heads(0, 0)
+        nc.sync.dma_start(
+            out=mask_rows[0:B * NB, :], in_=mask.rearrange("b (c p) -> (b c) p", p=P)
+        )
+        load_heads(0, 1)
         load_x(0)
         load_w(0)
-        load_heads(0, 1)
-        with nc.allow_non_contiguous_dma(reason="1024 mask values, one to a partition and block"):
-            nc.sync.dma_start(out=mask_sb[:], in_=mask.rearrange("b (c p) -> p b c", p=P))
+        load_heads(0, 2)
         load_w(1)
         load_heads(1, 0)
         load_x(1)
@@ -100,8 +118,9 @@ def tile_multiheadattention_pa_kernel(tc, Q, K, x, Wv, mask, out):
         row_on = {}
 
         def search(nat, b, f):
-            words = nat[b, f][:].bitcast(I32).rearrange("p c (h w) -> p (c h) w", h=HALF)
-            rows = NB * HALF
+            heads = LOADS[b][f][1]
+            words = nat[b, f][:].bitcast(I32).rearrange("p c (h w) -> p (c h) w", h=heads)
+            rows = NB * heads
             held = {}
 
             def join(level):
@@ -129,20 +148,20 @@ def tile_multiheadattention_pa_kernel(tc, Q, K, x, Wv, mask, out):
                 )
 
             def key_addend():
-                later[b, f] = keep.tile([P, NB, HALF], F32, name="later%d%d" % (b, f))
+                later[b, f] = keep.tile([P, NB, heads], F32, name="later%d%d" % (b, f))
                 nc.vector.tensor_scalar(
                     out=later[b, f][:].rearrange("p c h -> p (c h)"), in0=held["bits"][:],
                     scalar1=0.0, scalar2=ABSENT_KEY, op0=ALU.is_equal, op1=ALU.mult,
                 )
 
             def earlier_addend():
-                earlier[b, f] = keep.tile([P, NB, HALF], F32, name="earlier%d%d" % (b, f))
+                earlier[b, f] = keep.tile([P, NB, heads], F32, name="earlier%d%d" % (b, f))
                 nc.vector.tensor_scalar_add(
                     out=earlier[b, f][:], in0=later[b, f][:], scalar1=EARLIER_KEY
                 )
 
             def query_sign():
-                row_on[b, f] = keep.tile([P, NB, HALF], F32, name="row_on%d%d" % (b, f))
+                row_on[b, f] = keep.tile([P, NB, heads], F32, name="row_on%d%d" % (b, f))
                 nc.vector.tensor_single_scalar(
                     out=row_on[b, f][:].rearrange("p c h -> p (c h)"), in_=held["bits"][:],
                     scalar=0.0, op=ALU.is_gt,
@@ -151,7 +170,7 @@ def tile_multiheadattention_pa_kernel(tc, Q, K, x, Wv, mask, out):
             def query_mask():
                 nc.vector.tensor_tensor(
                     out=row_on[b, f][:], in0=row_on[b, f][:],
-                    in1=mask_sb[:, b, :].unsqueeze(2).to_broadcast([P, NB, HALF]), op=ALU.mult,
+                    in1=mask_sb[:, b, :].unsqueeze(2).to_broadcast([P, NB, heads]), op=ALU.mult,
                 )
 
             found = [key_addend, earlier_addend] if nat is k_nat else [query_sign, query_mask]
@@ -170,7 +189,7 @@ def tile_multiheadattention_pa_kernel(tc, Q, K, x, Wv, mask, out):
         v_scales = keep.tile([P, B * H, DH], U8, align_bytes=256)
 
         def turn_unit(nat, turned_sb, b, pair):
-            f, first = divmod(2 * pair, HALF)
+            f, first = load_of(b, 2 * pair)
             held = {}
 
             def fill():
@@ -222,7 +241,7 @@ def tile_multiheadattention_pa_kernel(tc, Q, K, x, Wv, mask, out):
             return pack_unit(words, x_codes[b][:, t, :], x_scales[b][:, t, :])
 
         def w_unit(r):
-            f, row = divmod(r, HALF)
+            f, row = divmod(r, H // 2)
             return pack_unit(w_nat[f][:].bitcast(F32)[:, row, :], w_codes[:, r, :], w_scales[:, r, :])
 
         v_ready = {}
@@ -274,7 +293,7 @@ def tile_multiheadattention_pa_kernel(tc, Q, K, x, Wv, mask, out):
 
         def make_addends(n, j):
             b, h = divmod(n, H)
-            f, hf = divmod(h, HALF)
+            f, hf = load_of(b, h)
             if j == 0:
                 addends[n] = soft.tile([P, NB, P], F32, bufs=3, name="addends")
             nc.gpsimd.tensor_scalar(
@@ -285,7 +304,7 @@ def tile_multiheadattention_pa_kernel(tc, Q, K, x, Wv, mask, out):
 
         def score(n, i):
             b, h = divmod(n, H)
-            f, hf = divmod(h, HALF)
+            f, hf = load_of(b, h)
             pair, hh = divmod(h, 2)
             scores[n, i] = psum.tile([P, T], F32, tag="scores", bufs=3, name="scores")
             nc.tensor.matmul(
@@ -369,7 +388,7 @@ def tile_multiheadattention_pa_kernel(tc, Q, K, x, Wv, mask, out):
 
         def weigh_rows(n, lo, hi):
             b, h = divmod(n, H)
-            f, hf = divmod(h, HALF)
+            f, hf = load_of(b, h)
             nc.gpsimd.tensor_tensor(
                 out=factor[n][:, lo:hi], in0=factor[n][:, lo:hi], in1=row_on[b, f][:, lo:hi, hf],
                 op=ALU.mult,
@@ -401,8 +420,16 @@ def tile_multiheadattention_pa_kernel(tc, Q, K, x, Wv, mask, out):
             units[NB * (t // 3) + 1 + t % 3] = x_unit(0, t)
             units[NB * (H - 3 + t) + 3] = x_unit(1, t)
 
-        searches = [search(k_nat, 0, 0)]
-        for run in searches[0]:
+        unread = psum.tile([P, T], F32, tag="sums", bufs=2)
+
+        def keep_clock(products):
+            for k in range(products):
+                nc.tensor.matmul(
+                    out=unread[:], lhsT=ident_bf[:], rhs=ones[:], start=True, stop=True
+                )
+
+        keep_clock(3)
+        for run in search(k_nat, 0, 0):
             run()
         for j in range(NB):
             make_addends(0, j)
@@ -410,9 +437,17 @@ def tile_multiheadattention_pa_kernel(tc, Q, K, x, Wv, mask, out):
             for run in stages:
                 run()
 
+        mask_turned = psum.tile([P, P], BF16, tag="turned", bufs=3)
+        nc.tensor.transpose(out=mask_turned[:], in_=mask_rows[:], identity=ident_bf[:])
+        nc.vector.tensor_copy(
+            out=mask_sb[:].rearrange("p b c -> p (b c)"), in_=mask_turned[:, 0:B * NB]
+        )
+
+        keep_clock(2)
+
         search_steps = []
         for nat, b, f in (
-            (q_nat, 0, 0), (k_nat, 0, 1), (q_nat, 0, 1),
+            (k_nat, 0, 1), (q_nat, 0, 0), (k_nat, 0, 2), (q_nat, 0, 1), (q_nat, 0, 2),
             (k_nat, 1, 0), (q_nat, 1, 0), (k_nat, 1, 1), (q_nat, 1, 1),
         ):
             search_steps.extend(search(nat, b, f))
@@ -421,6 +456,7 @@ def tile_multiheadattention_pa_kernel(tc, Q, K, x, Wv, mask, out):
         TILES = HEADS * NB
         weighed = 0
         finished = 0
+        done = 0
         score(0, 0)
         for step in range(TILES):
             n, i = divmod(step, NB)
@@ -453,8 +489,9 @@ def tile_multiheadattention_pa_kernel(tc, Q, K, x, Wv, mask, out):
                 exponent((step - 1) // NB, (step - 1) % NB)
             if n >= 1 and i % 2 == 0:
                 turn_e(n - 1, i, i + 2)
-            if step < len(search_steps):
-                search_steps[step]()
+            for run in search_steps[done:done + (2 if step < 2 * NB else 1)]:
+                run()
+                done += 1
             if n >= 1 and i == 2:
                 invert(n - 1, 0, NB)
             if n >= 1 and i == 3:

import math
from contextlib import ExitStack

import concourse.mybir as mybir
from concourse.masks import make_identity

F32 = mybir.dt.float32
BF16 = mybir.dt.bfloat16
U8 = mybir.dt.uint8
U32 = mybir.dt.uint32
I32 = mybir.dt.int32
FP8X4 = mybir.dt.float8_e4m3fn_x4
ALU = mybir.AluOpType
ACT = mybir.ActivationFunctionType
AX = mybir.AxisListType

P = 128
B, T, D, H = 2, 512, 1024, 8
DH = D // H
NB = T // P
PACK = 4
K_PASS = P * PACK
G = D // K_PASS
LOADS = (((0, 2), (2, 2), (4, 4)), ((0, 4), (4, 4)))
PAIRS = H // 2

SCALE = 1.0 / math.sqrt(DH)
ABSENT_KEY = (-(2.0**32) + 1.0) * math.sqrt(DH)
EARLIER_KEY = -round(10000.0 * math.sqrt(DH) * 128.0) / 128.0

NO_SIGN_BITS = 0x7FFF7FFF

FLOPS = 2 * B * T * D * D + 2 * (2 * B * H * T * T * DH)


def tile_multiheadattention_pa_kernel(tc, Q, K, x, Wv, mask, out):
    nc = tc.nc
    with ExitStack() as ctx:
        keep = ctx.enter_context(tc.tile_pool(name="keep", bufs=1))
        stage = ctx.enter_context(tc.tile_pool(name="stage", bufs=3))
        soft = ctx.enter_context(tc.tile_pool(name="soft", bufs=2))
        psum = ctx.enter_context(tc.psum_pool(name="psum", bufs=2))

        ident_bf = keep.tile([P, P], BF16, align_bytes=256)
        make_identity(nc, ident_bf[:])
        ident_f32 = keep.tile([P, P], F32, align_bytes=256)
        make_identity(nc, ident_f32[:])
        causal = keep.tile([P, P], F32)
        nc.gpsimd.memset(causal[:], EARLIER_KEY)
        nc.gpsimd.affine_select(
            out=causal[:], in_=causal[:], pattern=[[1, P]], compare_op=ALU.is_ge,
            fill=0.0, base=0, channel_multiplier=-1,
        )
        ones = keep.tile([P, T], BF16)
        nc.vector.memset(ones[:], 1.0)

        ctx.enter_context(tc.manual_schedule())

        k_nat = {}
        q_nat = {}
        x_nat = {}
        w_nat = {}
        for b in range(B):
            x_nat[b] = keep.tile([P, 2, 2 * D], BF16, align_bytes=256, name="x_nat%d" % b)
            for f in range(len(LOADS[b])):
                cols = LOADS[b][f][1] * DH
                k_nat[b, f] = keep.tile(
                    [P, NB, cols], BF16, align_bytes=256, name="k_nat%d%d" % (b, f)
                )
                q_nat[b, f] = keep.tile(
                    [P, NB, cols], BF16, align_bytes=256, name="q_nat%d%d" % (b, f)
                )
        for f in range(2):
            w_nat[f] = keep.tile([P, H // 2, D], BF16, align_bytes=256, name="w_nat%d" % f)
        mask_rows = keep.tile([P, P], BF16)
        mask_sb = keep.tile([P, B, NB], F32)
        nc.vector.memset(mask_rows[:], 0.0)

        def load_of(b, h):
            for f, (first, heads) in enumerate(LOADS[b]):
                if first <= h < first + heads:
                    return f, h - first

        def load_heads(b, f):
            first, heads = LOADS[b][f]
            cols = slice(first * DH, (first + heads) * DH)
            for nat, src in ((k_nat, K), (q_nat, Q)):
                nc.sync.dma_start(
                    out=nat[b, f][:], in_=src[b].rearrange("(c p) d -> p c d", p=P)[:, :, cols]
                )

        def load_x(b):
            nc.sync.dma_start(
                out=x_nat[b][:], in_=x[b].rearrange("(u p e) d -> p u (e d)", u=2, e=2)
            )

        def load_w(f):
            nc.sync.dma_start(
                out=w_nat[f][:],
                in_=Wv.rearrange("(r p) k -> p r k", p=P)[:, f * H // 2:(f + 1) * H // 2, :],
            )

        load_heads(0, 0)
        nc.sync.dma_start(
            out=mask_rows[0:B * NB, :], in_=mask.rearrange("b (c p) -> (b c) p", p=P)
        )
        load_heads(0, 1)
        load_x(0)
        load_w(0)
        load_heads(0, 2)
        load_w(1)
        load_heads(1, 0)
        load_x(1)
        load_heads(1, 1)

        later = {}
        earlier = {}
        row_on = {}

        def search(nat, b, f):
            heads = LOADS[b][f][1]
            words = nat[b, f][:].bitcast(I32).rearrange("p c (h w) -> p (c h) w", h=heads)
            rows = NB * heads
            held = {}

            def join(level):
                src = held["words"][:] if level else words
                width = DH // 4 >> level
                held["words"] = stage.tile(
                    [P, rows, width], I32, bufs=2, name="joined%d" % level
                )
                nc.vector.tensor_tensor(
                    out=held["words"][:], in0=src[:, :, 0:width], in1=src[:, :, width:2 * width],
                    op=ALU.bitwise_or,
                )

            def clear_signs():
                held["magnitudes"] = stage.tile([P, rows, DH // 8], I32, bufs=2, name="magnitudes")
                nc.vector.tensor_single_scalar(
                    out=held["magnitudes"][:], in_=held["words"][:], scalar=NO_SIGN_BITS,
                    op=ALU.bitwise_and,
                )

            def largest():
                held["bits"] = stage.tile([P, rows], F32, bufs=2, name="bits")
                nc.vector.tensor_reduce(
                    out=held["bits"][:], in_=held["magnitudes"][:], axis=AX.X, op=ALU.max
                )

            def key_addend():
                later[b, f] = keep.tile([P, NB, heads], F32, name="later%d%d" % (b, f))
                nc.vector.tensor_scalar(
                    out=later[b, f][:].rearrange("p c h -> p (c h)"), in0=held["bits"][:],
                    scalar1=0.0, scalar2=ABSENT_KEY, op0=ALU.is_equal, op1=ALU.mult,
                )

            def earlier_addend():
                earlier[b, f] = keep.tile([P, NB, heads], F32, name="earlier%d%d" % (b, f))
                nc.vector.tensor_scalar_add(
                    out=earlier[b, f][:], in0=later[b, f][:], scalar1=EARLIER_KEY
                )

            def query_sign():
                row_on[b, f] = keep.tile([P, NB, heads], F32, name="row_on%d%d" % (b, f))
                nc.vector.tensor_single_scalar(
                    out=row_on[b, f][:].rearrange("p c h -> p (c h)"), in_=held["bits"][:],
                    scalar=0.0, op=ALU.is_gt,
                )

            def query_mask():
                nc.vector.tensor_tensor(
                    out=row_on[b, f][:], in0=row_on[b, f][:],
                    in1=mask_sb[:, b, :].unsqueeze(2).to_broadcast([P, NB, heads]), op=ALU.mult,
                )

            found = [key_addend, earlier_addend] if nat is k_nat else [query_sign, query_mask]
            return [lambda: join(0), lambda: join(1), clear_signs, largest] + found

        kT = {}
        qT = {}
        x_codes = {}
        x_scales = {}
        for b in range(B):
            x_codes[b] = keep.tile([P, PACK, G * P], U32, align_bytes=256, name="x_codes%d" % b)
            x_scales[b] = keep.tile([P, PACK, G * P], U8, align_bytes=256, name="x_scales%d" % b)
        w_codes = keep.tile([P, H, G * P], U32, align_bytes=256)
        w_scales = keep.tile([P, H, G * P], U8, align_bytes=256)
        v_codes = keep.tile([P, B * H, DH], U32, align_bytes=256)
        v_scales = keep.tile([P, B * H, DH], U8, align_bytes=256)

        def turn_unit(nat, turned_sb, b, pair):
            f, first = load_of(b, 2 * pair)
            held = {}

            def fill():
                held["psum"] = psum.tile([P, 2, T], BF16, tag="turned", bufs=3, name="turned")
                for hh in range(2):
                    for c in range(NB):
                        nc.tensor.transpose(
                            out=held["psum"][:, hh, c * P:(c + 1) * P],
                            in_=nat[b, f][:, c, (first + hh) * DH:(first + hh + 1) * DH],
                            identity=ident_bf[:],
                        )

            def copy():
                which = "kT" if nat is k_nat else "qT"
                turned_sb[b, pair] = keep.tile([P, 2, T], BF16, align_bytes=256, name="%s%d%d" % (which, b, pair))
                nc.scalar.copy(out=turned_sb[b, pair][:], in_=held["psum"][:])

            return [fill, copy]

        def pack_unit(words, codes, scales):
            held = {}

            def fill():
                held["psum"] = psum.tile([P, G * 2, P], F32, tag="turned", bufs=3, name="turned")
                for q in range(G * 2):
                    nc.tensor.transpose(
                        out=held["psum"][:, q, :], in_=words[:, q * P:(q + 1) * P],
                        identity=ident_f32[:],
                    )

            def copy():
                held["sb"] = stage.tile([P, G, P, PACK], BF16, align_bytes=256, name="grouped")
                nc.scalar.copy(
                    out=held["sb"][:].bitcast(F32),
                    in_=held["psum"][:].rearrange("p (g u) r -> p g r u", g=G),
                )

            def quantise():
                nc.vector.quantize_mx(
                    out=codes.bitcast(FP8X4), scales=scales,
                    in_=held["sb"][:].rearrange("p g r t -> p (g r t)"),
                )

            return [fill, copy, quantise]

        def x_unit(b, t):
            u, e = divmod(t, 2)
            words = x_nat[b][:].bitcast(F32)[:, u, e * (D // 2):(e + 1) * (D // 2)]
            return pack_unit(words, x_codes[b][:, t, :], x_scales[b][:, t, :])

        def w_unit(r):
            f, row = divmod(r, H // 2)
            return pack_unit(w_nat[f][:].bitcast(F32)[:, row, :], w_codes[:, r, :], w_scales[:, r, :])

        v_ready = {}

        def v_unit(b, h):
            held = {}

            def fill():
                held["psum"] = psum.tile([P, PACK, DH], F32, tag="sums", bufs=2, name="v_acc")
                for t in range(PACK):
                    for g in range(G):
                        cols = slice(g * P, (g + 1) * P)
                        nc.tensor.matmul_mx(
                            out=held["psum"][:, t, :],
                            lhsT=x_codes[b][:, t, cols].bitcast(FP8X4),
                            lhsT_scale=x_scales[b][:, t, cols],
                            rhs=w_codes[:, h, cols].bitcast(FP8X4),
                            rhs_scale=w_scales[:, h, cols],
                            start=(g == 0), stop=(g == G - 1),
                        )

            def copy():
                held["sb"] = stage.tile([P, DH, PACK], BF16, align_bytes=256, name="v_grouped")
                nc.scalar.copy(
                    out=held["sb"][:], in_=held["psum"][:].rearrange("p t d -> p d t")
                )

            def quantise():
                nc.vector.quantize_mx(
                    out=v_codes[:, b * H + h, :].bitcast(FP8X4), scales=v_scales[:, b * H + h, :],
                    in_=held["sb"][:].rearrange("p d t -> p (d t)"),
                )
                v_ready[b, h] = True

            return [fill, copy, quantise]

        addends = {}
        e_sb = {}
        shift = {}
        rowsum = {}
        negated = {}
        e_turned = {}
        e_grouped = {}
        e_codes = {}
        e_scales = {}
        factor = {}
        scores = {}
        o_acc = {}

        def make_addends(n, j):
            b, h = divmod(n, H)
            f, hf = load_of(b, h)
            if j == 0:
                addends[n] = soft.tile([P, NB, P], F32, bufs=3, name="addends")
            nc.gpsimd.tensor_scalar(
                out=addends[n][:, j, :], in0=causal[:],
                scalar1=1.0, scalar2=later[b, f][:, j, hf:hf + 1],
                op0=ALU.mult, op1=ALU.add,
            )

        def score(n, i):
            b, h = divmod(n, H)
            f, hf = load_of(b, h)
            pair, hh = divmod(h, 2)
            scores[n, i] = psum.tile([P, T], F32, tag="scores", bufs=3, name="scores")
            nc.tensor.matmul(
                out=scores[n, i][:], lhsT=qT[b, pair][:, hh, i * P:(i + 1) * P],
                rhs=kT[b, pair][:, hh, :], start=True, stop=False,
            )
            for j in range(NB):
                if j == i:
                    addend = addends[n][:, j, :]
                else:
                    one_a_key = earlier if j < i else later
                    addend = one_a_key[b, f][:, j, hf:hf + 1].to_broadcast([P, P])
                nc.tensor.matmul(
                    out=scores[n, i][:, j * P:(j + 1) * P], lhsT=addend,
                    rhs=ident_f32[:], is_transpose=True, start=False, stop=(j == NB - 1),
                )

        def negate(n, i):
            if i == 0:
                shift[n] = soft.tile([P, NB], F32, bufs=3, name="shift")
            negated[n, i] = soft.tile([P, T], F32, bufs=4, name="negated")
            nc.vector.tensor_scalar(
                out=negated[n, i][:], in0=scores[n, i][:], scalar1=-SCALE, scalar2=None,
                op0=ALU.mult, op1=ALU.min, accum_out=shift[n][:, i:i + 1],
            )

        def exponent(n, i):
            if i == 0:
                e_sb[n] = soft.tile([P, NB, T], BF16, bufs=3, align_bytes=256, name="e_sb")
                rowsum[n] = soft.tile([P, NB], F32, bufs=4, name="rowsum")
            nc.scalar.activation(
                out=e_sb[n][:, i, :], in_=negated[n, i][:], func=ACT.Exp,
                bias=shift[n][:, i:i + 1], scale=-1.0, accum_out=rowsum[n][:, i:i + 1],
            )

        def turn_e(n, lo, hi):
            words = e_sb[n][:].bitcast(F32)
            e_turned[n, lo] = psum.tile([P, 2, (hi - lo) * P], F32, tag="turned", bufs=3, name="turned")
            for u in range(2):
                for i in range(lo, hi):
                    nc.tensor.transpose(
                        out=e_turned[n, lo][:, u, (i - lo) * P:(i - lo + 1) * P],
                        in_=words[:, i, u * P:(u + 1) * P], identity=ident_f32[:],
                    )

        def copy_e(n, lo, hi):
            if lo == 0:
                e_grouped[n] = soft.tile(
                    [P, NB * P, PACK], BF16, align_bytes=256, bufs=3, name="e_grouped"
                )
            nc.scalar.copy(
                out=e_grouped[n][:, lo * P:hi * P, :].bitcast(F32),
                in_=e_turned[n, lo][:].rearrange("p u i -> p i u"),
            )

        def quantise_e(n, lo, hi):
            if lo == 0:
                e_codes[n] = soft.tile([P, NB * P], U32, align_bytes=256, bufs=4, name="e_codes")
                e_scales[n] = soft.tile([P, NB * P], U8, align_bytes=256, bufs=4, name="e_scales")
            nc.vector.quantize_mx(
                out=e_codes[n][:, lo * P:hi * P].bitcast(FP8X4), scales=e_scales[n][:, lo * P:hi * P],
                in_=e_grouped[n][:, lo * P:hi * P, :].rearrange("p i t -> p (i t)"),
            )

        def weigh_v(n, lo, hi):
            o_acc[n, lo] = psum.tile([P, hi - lo, DH], F32, tag="sums", bufs=2, name="o_acc")
            for i in range(lo, hi):
                nc.tensor.matmul_mx(
                    out=o_acc[n, lo][:, i - lo, :],
                    lhsT=e_codes[n][:, i * P:(i + 1) * P].bitcast(FP8X4),
                    lhsT_scale=e_scales[n][:, i * P:(i + 1) * P],
                    rhs=v_codes[:, n, :].bitcast(FP8X4),
                    rhs_scale=v_scales[:, n, :],
                    start=True, stop=True,
                )

        def invert(n, lo, hi):
            if lo == 0:
                factor[n] = soft.tile([P, NB], F32, bufs=4, name="factor")
            nc.vector.reciprocal(out=factor[n][:, lo:hi], in_=rowsum[n][:, lo:hi])

        def weigh_rows(n, lo, hi):
            b, h = divmod(n, H)
            f, hf = load_of(b, h)
            nc.gpsimd.tensor_tensor(
                out=factor[n][:, lo:hi], in0=factor[n][:, lo:hi], in1=row_on[b, f][:, lo:hi, hf],
                op=ALU.mult,
            )

        def finish(n, lo, hi):
            b, h = divmod(n, H)
            o_sb = soft.tile([P, hi - lo, DH], F32, bufs=6)
            nc.vector.tensor_tensor(
                out=o_sb[:], in0=o_acc[n, lo][:],
                in1=factor[n][:, lo:hi].unsqueeze(2).to_broadcast([P, hi - lo, DH]), op=ALU.mult,
            )
            nc.sync.dma_start(
                out=out[b].rearrange("(i p) (h d) -> p i h d", p=P, h=H)[:, lo:hi, h, :], in_=o_sb[:]
            )

        units = {}
        for pair in range(1, B * PAIRS):
            units[NB * (2 * pair - 2)] = turn_unit(k_nat, kT, pair // PAIRS, pair % PAIRS)
            units[NB * (2 * pair - 1)] = turn_unit(q_nat, qT, pair // PAIRS, pair % PAIRS)
        for h in range(H):
            units[NB * (h + 1) + 2] = w_unit(h)
            units[NB * (h + 2) + 1] = v_unit(0, h)
            if h < 4:
                units[NB * (H + 2 + h // 2) + 1 + 2 * (h % 2)] = v_unit(1, h)
            else:
                units[NB * (H + h) + 1] = v_unit(1, h)
        for t in range(PACK):
            units[NB * (t // 3) + 1 + t % 3] = x_unit(0, t)
            units[NB * (H - 3 + t) + 3] = x_unit(1, t)

        unread = psum.tile([P, T], F32, tag="sums", bufs=2)

        def keep_clock(products):
            for k in range(products):
                nc.tensor.matmul(
                    out=unread[:], lhsT=ident_bf[:], rhs=ones[:], start=True, stop=True
                )

        keep_clock(3)
        for run in search(k_nat, 0, 0):
            run()
        for j in range(NB):
            make_addends(0, j)
        for stages in [turn_unit(k_nat, kT, 0, 0), turn_unit(q_nat, qT, 0, 0)]:
            for run in stages:
                run()

        mask_turned = psum.tile([P, P], BF16, tag="turned", bufs=3)
        nc.tensor.transpose(out=mask_turned[:], in_=mask_rows[:], identity=ident_bf[:])
        nc.vector.tensor_copy(
            out=mask_sb[:].rearrange("p b c -> p (b c)"), in_=mask_turned[:, 0:B * NB]
        )

        keep_clock(2)

        search_steps = []
        for nat, b, f in (
            (k_nat, 0, 1), (q_nat, 0, 0), (k_nat, 0, 2), (q_nat, 0, 1), (q_nat, 0, 2),
            (k_nat, 1, 0), (q_nat, 1, 0), (k_nat, 1, 1), (q_nat, 1, 1),
        ):
            search_steps.extend(search(nat, b, f))

        HEADS = B * H
        TILES = HEADS * NB
        weighed = 0
        finished = 0
        done = 0
        score(0, 0)
        for step in range(TILES):
            n, i = divmod(step, NB)
            if n + 1 < HEADS and i == 0:
                for j in range(NB):
                    make_addends(n + 1, j)

            ready = (weighed // H, weighed % H) in v_ready
            for lag in (2, 1):
                if step - lag in units and lag < len(units[step - lag]):
                    units[step - lag][lag]()
            if n >= 1 and i % 2 == 1:
                copy_e(n - 1, i - 1, i + 1)
            if n >= 2 and i == 0:
                quantise_e(n - 2, 0, NB)
            if finished < weighed:
                finish(finished, 0, NB)
                finished += 1

            if step + 1 < TILES:
                score((step + 1) // NB, (step + 1) % NB)
            if step in units:
                units[step][0]()
            if weighed < n - 1 and i % 2 == 1 and ready:
                weigh_v(weighed, 0, NB)
                weighed += 1

            negate(n, i)
            if step >= 1:
                exponent((step - 1) // NB, (step - 1) % NB)
            if n >= 1 and i % 2 == 0:
                turn_e(n - 1, i, i + 2)
            for run in search_steps[done:done + (2 if step < 2 * NB else 1)]:
                run()
                done += 1
            if n >= 1 and i == 2:
                invert(n - 1, 0, NB)
            if n >= 1 and i == 3:
                weigh_rows(n - 1, 0, NB)

        last = HEADS - 1
        parts = [(0, 2), (2, 3), (3, 4)]
        turn_e(last, *parts[0])
        exponent(last, NB - 1)
        quantise_e(last - 1, 0, NB)
        if finished < weighed:
            finish(finished, 0, NB)
            finished += 1
        copy_e(last, *parts[0])
        turn_e(last, *parts[1])
        copy_e(last, *parts[1])
        weigh_v(last - 1, 0, NB)
        turn_e(last, *parts[2])
        copy_e(last, *parts[2])
        quantise_e(last, *parts[0])
        invert(last, 0, NB)
        quantise_e(last, *parts[1])
        finish(last - 1, 0, NB)
        weigh_rows(last, 0, NB)
        weigh_v(last, *parts[0])
        quantise_e(last, *parts[2])
        finish(last, *parts[0])
        weigh_v(last, *parts[1])
        weigh_v(last, *parts[2])
        finish(last, *parts[1])
        finish(last, *parts[2])
